import numpy as np
import ml_dtypes


def mxq(x, axis, fmt="e4m3"):
    dtype, down = {"e4m3": (ml_dtypes.float8_e4m3fn, 7), "e5m2": (ml_dtypes.float8_e5m2, 14)}[fmt]
    v = np.moveaxis(np.asarray(x, np.float32).astype(ml_dtypes.bfloat16).astype(np.float64), axis, -1)
    blocks = v.reshape(v.shape[:-1] + (-1, 32))
    amax = np.abs(blocks).max(-1, keepdims=True)
    byte = np.maximum(np.where(amax > 0, np.frexp(amax)[1] - 1 + 127, 0) - down, 1)
    scale = np.exp2(byte - 127.0)
    codes = (blocks / scale).astype(np.float32).astype(dtype).astype(np.float64)
    return np.moveaxis((codes * scale).reshape(v.shape), -1, axis)


WIDE = False


def mx_kscale(k):
    if not WIDE:
        return np.ones(k)
    levels = np.array([10, -10, 5, -5, 0])
    a = np.random.permutation(np.resize(levels, k // 512 * 4)).reshape(k // 512, 4)
    idx = np.arange(k)
    return np.exp2(a[idx // 512, idx % 128 // 32])


BF16 = ml_dtypes.bfloat16


def bf(x):
    return np.asarray(x, np.float32).astype(BF16)


def f64(x):
    return np.asarray(x).astype(np.float64)


E2M1 = np.array([0.0, 0.5, 1.0, 1.5, 2.0, 3.0, 4.0, 6.0, -0.0, -0.5, -1.0, -1.5, -2.0, -3.0, -4.0, -6.0])


def pack_weight(w, fmt):
    k, n = w.shape
    w = f64(bf(w)).reshape(k // 32, 32, n)
    amax = np.abs(w).max(1)
    if fmt == "e4m3":
        byte = np.frexp(amax)[1] - 1 + 127 - 7
    else:
        mant, ex = np.frexp(amax / 6.0)
        byte = np.where(mant > 0.5, ex, ex - 1) + 127
    byte = np.clip(np.where(amax > 0, byte, 1), 1, 254)
    scaled = (w * np.exp2(127.0 - byte)[:, None, :]).reshape(k, n).astype(np.float32)
    by_word = np.ascontiguousarray(scaled.reshape(k // 512, 128, 4, n).transpose(0, 1, 3, 2))
    if fmt == "e4m3":
        words = by_word.astype(ml_dtypes.float8_e4m3fn).view(np.uint8)
    else:
        c = by_word.astype(ml_dtypes.float4_e2m1fn).view(np.uint8) & 0xF
        words = c[..., 0::2] | (c[..., 1::2] << 4)
    return np.ascontiguousarray(words), np.ascontiguousarray(byte.astype(np.uint8).reshape(k // 512, 16, n))


def unpack_weight(words, scales, fmt):
    g, p, n, _ = words.shape
    if fmt == "e4m3":
        vals = np.ascontiguousarray(words).view(ml_dtypes.float8_e4m3fn).astype(np.float64)
    else:
        nib = np.empty((g, p, n, 4), np.uint8)
        nib[..., 0::2] = words & 0xF
        nib[..., 1::2] = words >> 4
        vals = E2M1[nib]
    vals = vals * np.repeat(np.exp2(scales.astype(np.float64) - 127.0), 8, axis=1)[..., None]
    return vals.transpose(0, 1, 3, 2).reshape(g * 512, n)


B, I, H = 256, 16384, 512
G = 2 * H
EPS = 1e-5
FMT = "e4m3"


def ln(v):
    mu = v.mean(-1, keepdims=True)
    var = np.square(v - mu).mean(-1, keepdims=True)
    return (v - mu) / np.sqrt(var + EPS)


def sigmoid(v):
    return 1.0 / (1.0 + np.exp(-v))


def setup_inputs():
    s, t = mx_kscale(I), mx_kscale(H)
    x = bf(np.random.standard_normal((B, I)) * s)
    h = bf(np.random.standard_normal((B, H)) * t)
    irz_words, irz_scales = pack_weight((np.random.standard_normal((G, I)) / np.sqrt(I) / s).T, FMT)
    b_irz = bf(np.random.standard_normal(G) * 0.5)
    hrz_words, hrz_scales = pack_weight((np.random.standard_normal((G, H)) / np.sqrt(H) / t).T, FMT)
    b_hrz = bf(np.random.standard_normal(G) * 0.5)
    return {"x": x,
            "h": h,
            "W_irz_words": irz_words,
            "W_irz_scales": irz_scales,
            "b_irz": b_irz,
            "W_hrz_words": hrz_words,
            "W_hrz_scales": hrz_scales,
            "b_hrz": b_hrz}


def reference(x, h, W_irz_words, W_irz_scales, b_irz, W_hrz_words, W_hrz_scales, b_hrz):
    i_rz = ln((mxq(f64(x), 1, "e4m3") @ unpack_weight(W_irz_words, W_irz_scales, FMT)) + f64(b_irz))
    h_rz = ln((mxq(f64(h), 1, "e4m3") @ unpack_weight(W_hrz_words, W_hrz_scales, FMT)) + f64(b_hrz))
    return sigmoid(i_rz + h_rz)

@@ -1,0 +1,243 @@
+from contextlib import ExitStack
+
+import concourse.mybir as mybir
+from concourse.masks import make_identity
+
+F32 = mybir.dt.float32
+BF16 = mybir.dt.bfloat16
+I32 = mybir.dt.int32
+U32 = mybir.dt.uint32
+U8 = mybir.dt.uint8
+FP8X4 = mybir.dt.float8_e4m3fn_x4
+ALU = mybir.AluOpType
+ACT = mybir.ActivationFunctionType
+
+BATCH, IN_SIZE, HIDDEN = 256, 16384, 512
+GATES = 2 * HIDDEN
+EPS = 1e-5
+
+P = 128
+PACK = 4
+K_PASS = P * PACK
+WORDS_PASS = K_PASS // 2
+N_TILE = 512
+ROW_TILES = BATCH // P
+COL_TILES = GATES // N_TILE
+X_PASSES = IN_SIZE // K_PASS
+
+ROUND = 4
+ROUNDS = X_PASSES // ROUND
+W_ROUNDS_AHEAD = 3
+
+FLOPS = 2 * BATCH * (IN_SIZE + HIDDEN) * GATES
+
+
+def tile_layernormgrucell_pa_k_kernel(
+    tc, x, h, w_irz_words, w_irz_scales, b_irz, w_hrz_words, w_hrz_scales, b_hrz, out
+):
+    nc = tc.nc
+    with ExitStack() as ctx:
+        ctx.enter_context(tc.manual_schedule())
+
+        const = ctx.enter_context(tc.tile_pool(name="const", bufs=1))
+        x_pool = ctx.enter_context(tc.tile_pool(name="x", bufs=W_ROUNDS_AHEAD + 1))
+        w_pool = ctx.enter_context(tc.tile_pool(name="w", bufs=(W_ROUNDS_AHEAD + 1) * ROUND))
+        quant_pool = ctx.enter_context(tc.tile_pool(name="quant", bufs=2))
+        rows_pool = ctx.enter_context(tc.tile_pool(name="rows", bufs=ROW_TILES))
+        stat_pool = ctx.enter_context(tc.tile_pool(name="stat", bufs=2 * ROW_TILES))
+        sum_banks = ctx.enter_context(tc.psum_pool(name="sums", bufs=1))
+        spare_banks = ctx.enter_context(tc.psum_pool(name="spare", bufs=ROUND))
+
+        x_rows = x.rearrange("(m p) k -> p m k", p=P)
+        h_rows = h.rearrange("(m p) k -> p m k", p=P)
+        out_rows = out.rearrange("(m p) n -> p m n", p=P)
+        wi_words = w_irz_words.rearrange("g p n t -> g p (n t)").bitcast(I32)
+        wh_words = w_hrz_words.rearrange("g p n t -> g p (n t)").bitcast(I32)
+        wi_scales = w_irz_scales.bitcast(I32)
+        wh_scales = w_hrz_scales.bitcast(I32)
+
+        neg_half = const.tile([P, 1], F32)
+        nc.vector.memset(neg_half[:], -0.5)
+        ones = const.tile([P, P], BF16)
+        nc.vector.memset(ones[:], 1.0)
+        bias_rows = const.tile([P, 2 * GATES], BF16)
+        nc.vector.memset(bias_rows[:], 0.0)
+        nc.scalar.dma_start(out=bias_rows[0:1, 0:GATES], in_=b_irz.unsqueeze(0))
+        nc.scalar.dma_start(out=bias_rows[0:1, GATES : 2 * GATES], in_=b_hrz.unsqueeze(0))
+        identity = const.tile([P, P], F32)
+        make_identity(nc, identity[:])
+        table_warmer = const.tile([P, 1], F32)
+        nc.scalar.activation(out=table_warmer[:], in_=neg_half[:], func=ACT.Sigmoid)
+
+        w_planes = const.tile([P, ROUNDS + 1, GATES], U8, align_bytes=64)
+        nc.vector.memset(w_planes[:].rearrange("p r n -> p (r n)").bitcast(I32), 0)
+
+        def load_x(r):
+            x_sb = x_pool.tile([P, ROW_TILES, ROUND * K_PASS], BF16, name="x_sb")
+            k_cols = slice(r * ROUND * K_PASS, (r + 1) * ROUND * K_PASS)
+            nc.sync.dma_start(out=x_sb[:], in_=x_rows[:, :, k_cols])
+            return x_sb
+
+        def load_w(g):
+            w_sb = w_pool.tile([P, GATES], U32, name="w_sb", align_bytes=64)
+            nc.sync.dma_start(out=w_sb[:].bitcast(I32), in_=wi_words[g])
+            return w_sb
+
+        def load_scale_planes(r):
+            for quadrant in range(4):
+                nc.sync.dma_start(
+                    out=w_planes[32 * quadrant : 32 * quadrant + 16, r, :].bitcast(I32),
+                    in_=wi_scales[r * ROUND : (r + 1) * ROUND, 4 * quadrant : 4 * quadrant + 4, :],
+                )
+
+        x_tiles = {}
+        w_tiles = {}
+
+        def load_round(r):
+            if r + 1 < ROUNDS:
+                x_tiles[r + 1] = load_x(r + 1)
+            for g in range(r * ROUND, (r + 1) * ROUND):
+                w_tiles[g] = load_w(g)
+
+        h_sb = const.tile([P, ROW_TILES, HIDDEN], BF16)
+        nc.sync.dma_start(out=h_sb[:], in_=h_rows)
+        wh_sb = const.tile([P, GATES], U32, align_bytes=64)
+        nc.sync.dma_start(out=wh_sb[:].bitcast(I32), in_=wh_words[0])
+        for quadrant in range(4):
+            nc.sync.dma_start(
+                out=w_planes[32 * quadrant : 32 * quadrant + 4, ROUNDS, :].bitcast(I32),
+                in_=wh_scales[0, 4 * quadrant : 4 * quadrant + 4, :],
+            )
+        x_tiles[0] = load_x(0)
+        for r in range(ROUNDS):
+            load_scale_planes(r)
+        for r in range(W_ROUNDS_AHEAD):
+            load_round(r)
+
+        def transpose_and_quantise(rows_sb, passes, label):
+            words = rows_sb[:].bitcast(F32)
+            grouped = quant_pool.tile(
+                [P, passes * BATCH * PACK], BF16, name=label + "_grouped", align_bytes=64
+            )
+            grouped_words = grouped[:].bitcast(F32).rearrange("p (g c u) -> p g c u", g=passes, u=2)
+            for g in range(passes):
+                turned = spare_banks.tile([P, 2, BATCH], F32, name="turned", tag="spare")
+                for u in range(2):
+                    for m in range(ROW_TILES):
+                        nc.tensor.transpose(
+                            turned[:, u, m * P : (m + 1) * P],
+                            words[:, m, g * WORDS_PASS + u : (g + 1) * WORDS_PASS : 2],
+                            identity[:],
+                        )
+                nc.scalar.copy(out=grouped_words[:, g], in_=turned[:].rearrange("p u c -> p c u"))
+            codes = quant_pool.tile([P, passes * BATCH], U32, name=label + "_codes", align_bytes=64)
+            scales = quant_pool.tile([P, passes * BATCH], U8, name=label + "_scales", align_bytes=64)
+            nc.vector.quantize_mx(out=codes[:].bitcast(FP8X4), scales=scales[:], in_=grouped[:])
+            return codes, scales
+
+        def new_sums():
+            return [
+                [
+                    sum_banks.tile([P, N_TILE], F32, name="sums_%d_%d" % (m, n))
+                    for n in range(COL_TILES)
+                ]
+                for m in range(ROW_TILES)
+            ]
+
+        def multiply_pass(sums, quantised, g_local, w_sb, plane, first, last):
+            codes, scales = quantised
+            for m in range(ROW_TILES):
+                rows = slice(g_local * BATCH + m * P, g_local * BATCH + (m + 1) * P)
+                for n in range(COL_TILES):
+                    cols = slice(n * N_TILE, (n + 1) * N_TILE)
+                    nc.tensor.matmul_mx(
+                        out=sums[m][n][:],
+                        lhsT=codes[:, rows].bitcast(FP8X4),
+                        lhsT_scale=scales[:, rows],
+                        rhs=w_sb[:, cols].bitcast(FP8X4),
+                        rhs_scale=plane[:, cols],
+                        start=first,
+                        stop=last,
+                    )
+
+        def add_bias(sums_m, bias_cols):
+            v = rows_pool.tile([P, GATES], F32, name="v")
+            for n in range(COL_TILES):
+                cols = slice(n * N_TILE, (n + 1) * N_TILE)
+                nc.vector.tensor_tensor(
+                    out=v[:, cols], in0=sums_m[n][:], in1=bias_cols[:, cols], op=ALU.add
+                )
+            return v
+
+        def row_statistics(v):
+            stats = stat_pool.tile([P, COL_TILES, 6], F32, name="stats")
+            for n in range(COL_TILES):
+                nc.vector.bn_stats(out=stats[:, n, :], in_=v[:, n * N_TILE : (n + 1) * N_TILE])
+            mean_var = stat_pool.tile([P, 2], F32, name="mean_var")
+            nc.vector.bn_aggr(out=mean_var[:], in_=stats[:].rearrange("p n s -> p (n s)"))
+            var_eps = stat_pool.tile([P, 1], F32, name="var_eps")
+            nc.vector.tensor_scalar_add(var_eps[:], mean_var[:, 1:2], EPS)
+            rstd = stat_pool.tile([P, 1], F32, name="rstd")
+            nc.gpsimd.tensor_tensor(out=rstd[:], in0=var_eps[:], in1=neg_half[:], op=ALU.pow)
+            shift = stat_pool.tile([P, 1], F32, name="shift")
+            nc.vector.scalar_tensor_tensor(
+                out=shift[:], in0=mean_var[:, 0:1], scalar=-1.0, in1=rstd[:],
+                op0=ALU.mult, op1=ALU.mult,
+            )
+            return rstd, shift
+
+        h_quantised = transpose_and_quantise(h_sb, 1, "h")
+
+        bias = const.tile([P, 2 * GATES], F32)
+        for c in range(2 * COL_TILES):
+            cols = slice(c * N_TILE, (c + 1) * N_TILE)
+            spread = spare_banks.tile([P, N_TILE], F32, name="spread", tag="spare")
+            nc.tensor.matmul(out=spread[:], lhsT=ones[:], rhs=bias_rows[:, cols], start=True, stop=True)
+            nc.scalar.copy(out=bias[:, cols], in_=spread[:])
+
+        h_sums = new_sums()
+        multiply_pass(h_sums, h_quantised, 0, wh_sb, w_planes[:, ROUNDS, :], True, True)
+        h_v = [add_bias(h_sums[m], bias[:, GATES : 2 * GATES]) for m in range(ROW_TILES)]
+
+        x_quantised = {0: transpose_and_quantise(x_tiles[0], ROUND, "x")}
+
+        h_norm = []
+        for m in range(ROW_TILES):
+            rstd, shift = row_statistics(h_v[m])
+            h_norm_m = rows_pool.tile([P, GATES], F32, name="h_norm")
+            nc.vector.tensor_scalar(
+                out=h_norm_m[:], in0=h_v[m][:], scalar1=rstd[:], scalar2=shift[:],
+                op0=ALU.mult, op1=ALU.add,
+            )
+            h_norm.append(h_norm_m)
+
+        x_sums = new_sums()
+        for r in range(ROUNDS):
+            if r + W_ROUNDS_AHEAD < ROUNDS:
+                load_round(r + W_ROUNDS_AHEAD)
+            if r + 1 < ROUNDS:
+                x_quantised[r + 1] = transpose_and_quantise(x_tiles[r + 1], ROUND, "x")
+            for j in range(ROUND):
+                g = r * ROUND + j
+                multiply_pass(
+                    x_sums, x_quantised[r], j, w_tiles[g], w_planes[4 * j : P, r, :],
+                    g == 0, g == X_PASSES - 1,
+                )
+
+        x_v = []
+        x_stats = []
+        for m in range(ROW_TILES):
+            x_v.append(add_bias(x_sums[m], bias[:, 0:GATES]))
+            x_stats.append(row_statistics(x_v[m]))
+        for m in range(ROW_TILES):
+            rstd, shift = x_stats[m]
+            z = rows_pool.tile([P, GATES], F32, name="z")
+            gates = rows_pool.tile([P, GATES], F32, name="gates")
+            for n in range(COL_TILES):
+                cols = slice(n * N_TILE, (n + 1) * N_TILE)
+                nc.vector.scalar_tensor_tensor(
+                    out=z[:, cols], in0=x_v[m][:, cols], scalar=rstd[:], in1=h_norm[m][:, cols],
+                    op0=ALU.mult, op1=ALU.add,
+                )
+                nc.scalar.activation(out=gates[:, cols], in_=z[:, cols], func=ACT.Sigmoid, bias=shift[:])
+                nc.sync.dma_start(out=out_rows[:, m, cols], in_=gates[:, cols])

@@ -28,6 +28,7 @@ X_PASSES = IN_SIZE // K_PASS
 ROUND = 4
 ROUNDS = X_PASSES // ROUND
 W_ROUNDS_AHEAD = 3
+PLANE_ROUNDS_FIRST = 2
 
 FLOPS = 2 * BATCH * (IN_SIZE + HIDDEN) * GATES
 
@@ -53,7 +54,7 @@ def tile_layernormgrucell_pa_k_kernel(
         out_rows = out.rearrange("(m p) n -> p m n", p=P)
         wi_words = w_irz_words.rearrange("g p n t -> g p (n t)").bitcast(I32)
         wh_words = w_hrz_words.rearrange("g p n t -> g p (n t)").bitcast(I32)
-        wi_scales = w_irz_scales.bitcast(I32)
+        wi_scales = w_irz_scales.bitcast(F32)
         wh_scales = w_hrz_scales.bitcast(I32)
 
         neg_half = const.tile([P, 1], F32)
@@ -85,8 +86,8 @@ def tile_layernormgrucell_pa_k_kernel(
 
         def load_scale_planes(r):
             for quadrant in range(4):
-                nc.sync.dma_start(
-                    out=w_planes[32 * quadrant : 32 * quadrant + 16, r, :].bitcast(I32),
+                nc.gpsimd.dma_start(
+                    out=w_planes[32 * quadrant : 32 * quadrant + 16, r, :].bitcast(F32),
                     in_=wi_scales[r * ROUND : (r + 1) * ROUND, 4 * quadrant : 4 * quadrant + 4, :],
                 )
 
@@ -109,7 +110,7 @@ def tile_layernormgrucell_pa_k_kernel(
                 in_=wh_scales[0, 4 * quadrant : 4 * quadrant + 4, :],
             )
         x_tiles[0] = load_x(0)
-        for r in range(ROUNDS):
+        for r in range(PLANE_ROUNDS_FIRST):
             load_scale_planes(r)
         for r in range(W_ROUNDS_AHEAD):
             load_round(r)
@@ -210,6 +211,8 @@ def tile_layernormgrucell_pa_k_kernel(
                 op0=ALU.mult, op1=ALU.add,
             )
             h_norm.append(h_norm_m)
+        for r in range(PLANE_ROUNDS_FIRST, ROUNDS):
+            load_scale_planes(r)
 
         x_sums = new_sums()
         for r in range(ROUNDS):

@@ -19,7 +19,6 @@ EPS = 1e-5
 P = 128
 PACK = 4
 K_PASS = P * PACK
-WORDS_PASS = K_PASS // 2
 N_TILE = 512
 ROW_TILES = BATCH // P
 COL_TILES = GATES // N_TILE
@@ -116,7 +115,13 @@ def tile_layernormgrucell_pa_k_kernel(
             load_round(r)
 
         def transpose_and_quantise(rows_sb, passes, label):
-            words = rows_sb[:].bitcast(F32)
+            sorted_words = quant_pool.tile(
+                [P, ROW_TILES * passes, 2, P], F32, name=label + "_sorted_words"
+            )
+            nc.vector.tensor_copy(
+                out=sorted_words[:],
+                in_=rows_sb[:].bitcast(F32).rearrange("b m (g p u) -> b (m g) u p", g=passes, u=2),
+            )
             grouped = quant_pool.tile(
                 [P, passes * BATCH * PACK], BF16, name=label + "_grouped", align_bytes=64
             )
@@ -127,7 +132,7 @@ def tile_layernormgrucell_pa_k_kernel(
                     for m in range(ROW_TILES):
                         nc.tensor.transpose(
                             turned[:, u, m * P : (m + 1) * P],
-                            words[:, m, g * WORDS_PASS + u : (g + 1) * WORDS_PASS : 2],
+                            sorted_words[:, m * passes + g, u, :],
                             identity[:],
                         )
                 nc.scalar.copy(out=grouped_words[:, g], in_=turned[:].rearrange("p u c -> p c u"))

@@ -26,6 +26,7 @@ X_PASSES = IN_SIZE // K_PASS
 
 ROUND = 4
 ROUNDS = X_PASSES // ROUND
+X_ROUNDS_AHEAD = 2
 W_ROUNDS_AHEAD = 3
 PLANE_ROUNDS_FIRST = 2
 
@@ -40,7 +41,7 @@ def tile_layernormgrucell_pa_k_kernel(
         ctx.enter_context(tc.manual_schedule())
 
         const = ctx.enter_context(tc.tile_pool(name="const", bufs=1))
-        x_pool = ctx.enter_context(tc.tile_pool(name="x", bufs=W_ROUNDS_AHEAD + 1))
+        x_pool = ctx.enter_context(tc.tile_pool(name="x", bufs=W_ROUNDS_AHEAD + X_ROUNDS_AHEAD))
         w_pool = ctx.enter_context(tc.tile_pool(name="w", bufs=(W_ROUNDS_AHEAD + 1) * ROUND))
         quant_pool = ctx.enter_context(tc.tile_pool(name="quant", bufs=2))
         rows_pool = ctx.enter_context(tc.tile_pool(name="rows", bufs=ROW_TILES))
@@ -54,23 +55,21 @@ def tile_layernormgrucell_pa_k_kernel(
         wi_words = w_irz_words.rearrange("g p n t -> g p (n t)").bitcast(I32)
         wh_words = w_hrz_words.rearrange("g p n t -> g p (n t)").bitcast(I32)
         wi_scales = w_irz_scales.bitcast(F32)
-        wh_scales = w_hrz_scales.bitcast(I32)
+        wh_scales = w_hrz_scales.bitcast(F32)
 
-        neg_half = const.tile([P, 1], F32)
-        nc.vector.memset(neg_half[:], -0.5)
-        ones = const.tile([P, P], BF16)
-        nc.vector.memset(ones[:], 1.0)
-        bias_rows = const.tile([P, 2 * GATES], BF16)
-        nc.vector.memset(bias_rows[:], 0.0)
-        nc.scalar.dma_start(out=bias_rows[0:1, 0:GATES], in_=b_irz.unsqueeze(0))
-        nc.scalar.dma_start(out=bias_rows[0:1, GATES : 2 * GATES], in_=b_hrz.unsqueeze(0))
-        identity = const.tile([P, P], F32)
-        make_identity(nc, identity[:])
-        table_warmer = const.tile([P, 1], F32)
-        nc.scalar.activation(out=table_warmer[:], in_=neg_half[:], func=ACT.Sigmoid)
+        def col_tile(n):
+            return slice(n * N_TILE, (n + 1) * N_TILE)
 
         w_planes = const.tile([P, ROUNDS + 1, GATES], U8, align_bytes=64)
         nc.vector.memset(w_planes[:].rearrange("p r n -> p (r n)").bitcast(I32), 0)
+        bias_rows = const.tile([P, 2 * GATES], BF16)
+        nc.vector.memset(bias_rows[:].bitcast(I32), 0)
+        ones = const.tile([P, P], BF16)
+        nc.vector.memset(ones[:], 1.0)
+        neg_half = const.tile([P, ROW_TILES], F32)
+        nc.vector.memset(neg_half[:], -0.5)
+        identity = const.tile([P, P], F32)
+        make_identity(nc, identity[:])
 
         def load_x(r):
             x_sb = x_pool.tile([P, ROW_TILES, ROUND * K_PASS], BF16, name="x_sb")
@@ -94,8 +93,8 @@ def tile_layernormgrucell_pa_k_kernel(
         w_tiles = {}
 
         def load_round(r):
-            if r + 1 < ROUNDS:
-                x_tiles[r + 1] = load_x(r + 1)
+            if r + X_ROUNDS_AHEAD < ROUNDS:
+                x_tiles[r + X_ROUNDS_AHEAD] = load_x(r + X_ROUNDS_AHEAD)
             for g in range(r * ROUND, (r + 1) * ROUND):
                 w_tiles[g] = load_w(g)
 
@@ -103,18 +102,25 @@ def tile_layernormgrucell_pa_k_kernel(
         nc.sync.dma_start(out=h_sb[:], in_=h_rows)
         wh_sb = const.tile([P, GATES], U32, align_bytes=64)
         nc.sync.dma_start(out=wh_sb[:].bitcast(I32), in_=wh_words[0])
-        for quadrant in range(4):
-            nc.sync.dma_start(
-                out=w_planes[32 * quadrant : 32 * quadrant + 4, ROUNDS, :].bitcast(I32),
-                in_=wh_scales[0, 4 * quadrant : 4 * quadrant + 4, :],
-            )
-        x_tiles[0] = load_x(0)
-        for r in range(PLANE_ROUNDS_FIRST):
-            load_scale_planes(r)
+        for r in range(X_ROUNDS_AHEAD):
+            x_tiles[r] = load_x(r)
         for r in range(W_ROUNDS_AHEAD):
             load_round(r)
 
-        def transpose_and_quantise(rows_sb, passes, label):
+        nc.scalar.dma_start(out=bias_rows[0:1, 0:GATES], in_=b_irz.unsqueeze(0))
+        nc.scalar.dma_start(out=bias_rows[0:1, GATES : 2 * GATES], in_=b_hrz.unsqueeze(0))
+        for quadrant in range(4):
+            nc.scalar.dma_start(
+                out=w_planes[32 * quadrant : 32 * quadrant + 4, ROUNDS, :].bitcast(F32),
+                in_=wh_scales[0, 4 * quadrant : 4 * quadrant + 4, :],
+            )
+        for r in range(PLANE_ROUNDS_FIRST):
+            load_scale_planes(r)
+
+        table_warmer = const.tile([P, 1], F32)
+        nc.scalar.activation(out=table_warmer[:], in_=neg_half[:, 0:1], func=ACT.Sigmoid)
+
+        def sort_words(rows_sb, passes, label):
             sorted_words = quant_pool.tile(
                 [P, ROW_TILES * passes, 2, P], F32, name=label + "_sorted_words"
             )
@@ -122,6 +128,9 @@ def tile_layernormgrucell_pa_k_kernel(
                 out=sorted_words[:],
                 in_=rows_sb[:].bitcast(F32).rearrange("b m (g p u) -> b (m g) u p", g=passes, u=2),
             )
+            return sorted_words
+
+        def transpose_and_quantise(sorted_words, passes, label):
             grouped = quant_pool.tile(
                 [P, passes * BATCH * PACK], BF16, name=label + "_grouped", align_bytes=64
             )
@@ -150,72 +159,90 @@ def tile_layernormgrucell_pa_k_kernel(
                 for m in range(ROW_TILES)
             ]
 
-        def multiply_pass(sums, quantised, g_local, w_sb, plane, first, last):
+        def multiply(sums, quantised, g_local, n, w_sb, plane, first, last):
             codes, scales = quantised
             for m in range(ROW_TILES):
                 rows = slice(g_local * BATCH + m * P, g_local * BATCH + (m + 1) * P)
-                for n in range(COL_TILES):
-                    cols = slice(n * N_TILE, (n + 1) * N_TILE)
-                    nc.tensor.matmul_mx(
-                        out=sums[m][n][:],
-                        lhsT=codes[:, rows].bitcast(FP8X4),
-                        lhsT_scale=scales[:, rows],
-                        rhs=w_sb[:, cols].bitcast(FP8X4),
-                        rhs_scale=plane[:, cols],
-                        start=first,
-                        stop=last,
-                    )
-
-        def add_bias(sums_m, bias_cols):
-            v = rows_pool.tile([P, GATES], F32, name="v")
-            for n in range(COL_TILES):
-                cols = slice(n * N_TILE, (n + 1) * N_TILE)
-                nc.vector.tensor_tensor(
-                    out=v[:, cols], in0=sums_m[n][:], in1=bias_cols[:, cols], op=ALU.add
+                nc.tensor.matmul_mx(
+                    out=sums[m][n][:],
+                    lhsT=codes[:, rows].bitcast(FP8X4),
+                    lhsT_scale=scales[:, rows],
+                    rhs=w_sb[:, col_tile(n)].bitcast(FP8X4),
+                    rhs_scale=plane[:, col_tile(n)],
+                    start=first,
+                    stop=last,
                 )
-            return v
 
-        def row_statistics(v):
-            stats = stat_pool.tile([P, COL_TILES, 6], F32, name="stats")
-            for n in range(COL_TILES):
-                nc.vector.bn_stats(out=stats[:, n, :], in_=v[:, n * N_TILE : (n + 1) * N_TILE])
-            mean_var = stat_pool.tile([P, 2], F32, name="mean_var")
-            nc.vector.bn_aggr(out=mean_var[:], in_=stats[:].rearrange("p n s -> p (n s)"))
-            var_eps = stat_pool.tile([P, 1], F32, name="var_eps")
-            nc.vector.tensor_scalar_add(var_eps[:], mean_var[:, 1:2], EPS)
-            rstd = stat_pool.tile([P, 1], F32, name="rstd")
+        def new_rows(label):
+            return [rows_pool.tile([P, GATES], F32, name=label) for m in range(ROW_TILES)]
+
+        def new_stats():
+            return [
+                stat_pool.tile([P, COL_TILES, 6], F32, name="stats") for m in range(ROW_TILES)
+            ]
+
+        def add_bias(v, sums, bias_cols, n):
+            for m in range(ROW_TILES):
+                nc.vector.tensor_tensor(
+                    out=v[m][:, col_tile(n)], in0=sums[m][n][:], in1=bias_cols[:, col_tile(n)],
+                    op=ALU.add,
+                )
+
+        def measure(stats, v, n):
+            for m in range(ROW_TILES):
+                nc.vector.bn_stats(out=stats[m][:, n, :], in_=v[m][:, col_tile(n)])
+
+        def scale_and_shift(stats):
+            mean_var = stat_pool.tile([P, ROW_TILES, 2], F32, name="mean_var")
+            for m in range(ROW_TILES):
+                nc.vector.bn_aggr(
+                    out=mean_var[:, m, :], in_=stats[m][:].rearrange("p n s -> p (n s)")
+                )
+            var_eps = stat_pool.tile([P, ROW_TILES], F32, name="var_eps")
+            nc.vector.tensor_scalar_add(var_eps[:], mean_var[:, :, 1], EPS)
+            rstd = stat_pool.tile([P, ROW_TILES], F32, name="rstd")
             nc.gpsimd.tensor_tensor(out=rstd[:], in0=var_eps[:], in1=neg_half[:], op=ALU.pow)
-            shift = stat_pool.tile([P, 1], F32, name="shift")
+            shift = stat_pool.tile([P, ROW_TILES], F32, name="shift")
             nc.vector.scalar_tensor_tensor(
-                out=shift[:], in0=mean_var[:, 0:1], scalar=-1.0, in1=rstd[:],
+                out=shift[:], in0=mean_var[:, :, 0], scalar=-1.0, in1=rstd[:],
                 op0=ALU.mult, op1=ALU.mult,
             )
             return rstd, shift
 
-        h_quantised = transpose_and_quantise(h_sb, 1, "h")
+        h_quantised = transpose_and_quantise(sort_words(h_sb, 1, "h"), 1, "h")
 
         bias = const.tile([P, 2 * GATES], F32)
         for c in range(2 * COL_TILES):
-            cols = slice(c * N_TILE, (c + 1) * N_TILE)
             spread = spare_banks.tile([P, N_TILE], F32, name="spread", tag="spare")
-            nc.tensor.matmul(out=spread[:], lhsT=ones[:], rhs=bias_rows[:, cols], start=True, stop=True)
-            nc.scalar.copy(out=bias[:, cols], in_=spread[:])
+            nc.tensor.matmul(
+                out=spread[:], lhsT=ones[:], rhs=bias_rows[:, col_tile(c)], start=True, stop=True
+            )
+            nc.scalar.copy(out=bias[:, col_tile(c)], in_=spread[:])
+        x_bias = bias[:, 0:GATES]
+        h_bias = bias[:, GATES : 2 * GATES]
 
         h_sums = new_sums()
-        multiply_pass(h_sums, h_quantised, 0, wh_sb, w_planes[:, ROUNDS, :], True, True)
-        h_v = [add_bias(h_sums[m], bias[:, GATES : 2 * GATES]) for m in range(ROW_TILES)]
+        for n in range(COL_TILES):
+            multiply(h_sums, h_quantised, 0, n, wh_sb, w_planes[:, ROUNDS, :], True, True)
 
-        x_quantised = {0: transpose_and_quantise(x_tiles[0], ROUND, "x")}
+        x_sorted = {0: sort_words(x_tiles[0], ROUND, "x")}
+        h_v = new_rows("v")
+        for n in range(COL_TILES):
+            add_bias(h_v, h_sums, h_bias, n)
+        x_sorted[1] = sort_words(x_tiles[1], ROUND, "x")
+        x_quantised = {0: transpose_and_quantise(x_sorted[0], ROUND, "x")}
 
-        h_norm = []
+        h_stats = new_stats()
+        for n in range(COL_TILES):
+            measure(h_stats, h_v, n)
+        h_norm = new_rows("h_norm")
+        h_rstd, h_shift = scale_and_shift(h_stats)
         for m in range(ROW_TILES):
-            rstd, shift = row_statistics(h_v[m])
-            h_norm_m = rows_pool.tile([P, GATES], F32, name="h_norm")
             nc.vector.tensor_scalar(
-                out=h_norm_m[:], in0=h_v[m][:], scalar1=rstd[:], scalar2=shift[:],
+                out=h_norm[m][:], in0=h_v[m][:],
+                scalar1=h_rstd[:, m : m + 1], scalar2=h_shift[:, m : m + 1],
                 op0=ALU.mult, op1=ALU.add,
             )
-            h_norm.append(h_norm_m)
         for r in range(PLANE_ROUNDS_FIRST, ROUNDS):
             load_scale_planes(r)
 
@@ -223,29 +250,38 @@ def tile_layernormgrucell_pa_k_kernel(
         for r in range(ROUNDS):
             if r + W_ROUNDS_AHEAD < ROUNDS:
                 load_round(r + W_ROUNDS_AHEAD)
+            if r + 2 < ROUNDS:
+                x_sorted[r + 2] = sort_words(x_tiles[r + 2], ROUND, "x")
             if r + 1 < ROUNDS:
-                x_quantised[r + 1] = transpose_and_quantise(x_tiles[r + 1], ROUND, "x")
-            for j in range(ROUND):
+                x_quantised[r + 1] = transpose_and_quantise(x_sorted[r + 1], ROUND, "x")
+            if r + 1 < ROUNDS:
+                steps = [(j, n) for j in range(ROUND) for n in range(COL_TILES)]
+            else:
+                steps = [(j, n) for n in range(COL_TILES) for j in range(ROUND)]
+            for j, n in steps:
                 g = r * ROUND + j
-                multiply_pass(
-                    x_sums, x_quantised[r], j, w_tiles[g], w_planes[4 * j : P, r, :],
+                multiply(
+                    x_sums, x_quantised[r], j, n, w_tiles[g], w_planes[4 * j : P, r, :],
                     g == 0, g == X_PASSES - 1,
                 )
 
-        x_v = []
-        x_stats = []
+        x_v = new_rows("v")
+        x_stats = new_stats()
+        for n in range(COL_TILES):
+            add_bias(x_v, x_sums, x_bias, n)
+            measure(x_stats, x_v, n)
+        x_rstd, x_shift = scale_and_shift(x_stats)
+        z = new_rows("z")
+        gates = new_rows("gates")
         for m in range(ROW_TILES):
-            x_v.append(add_bias(x_sums[m], bias[:, 0:GATES]))
-            x_stats.append(row_statistics(x_v[m]))
-        for m in range(ROW_TILES):
-            rstd, shift = x_stats[m]
-            z = rows_pool.tile([P, GATES], F32, name="z")
-            gates = rows_pool.tile([P, GATES], F32, name="gates")
             for n in range(COL_TILES):
-                cols = slice(n * N_TILE, (n + 1) * N_TILE)
+                cols = col_tile(n)
                 nc.vector.scalar_tensor_tensor(
-                    out=z[:, cols], in0=x_v[m][:, cols], scalar=rstd[:], in1=h_norm[m][:, cols],
-                    op0=ALU.mult, op1=ALU.add,
+                    out=z[m][:, cols], in0=x_v[m][:, cols], scalar=x_rstd[:, m : m + 1],
+                    in1=h_norm[m][:, cols], op0=ALU.mult, op1=ALU.add,
                 )
-                nc.scalar.activation(out=gates[:, cols], in_=z[:, cols], func=ACT.Sigmoid, bias=shift[:])
-                nc.sync.dma_start(out=out_rows[:, m, cols], in_=gates[:, cols])
+                nc.scalar.activation(
+                    out=gates[m][:, cols], in_=z[m][:, cols], func=ACT.Sigmoid,
+                    bias=x_shift[:, m : m + 1],
+                )
+                nc.sync.dma_start(out=out_rows[:, m, cols], in_=gates[m][:, cols])

@@ -23,12 +23,18 @@ N_TILE = 512
 ROW_TILES = BATCH // P
 COL_TILES = GATES // N_TILE
 X_PASSES = IN_SIZE // K_PASS
+PLANE_GROUP = 4
+PLANE_GROUPS = X_PASSES // PLANE_GROUP
 
-ROUND = 4
-ROUNDS = X_PASSES // ROUND
-X_ROUNDS_AHEAD = 2
-W_ROUNDS_AHEAD = 3
-PLANE_ROUNDS_FIRST = 2
+ROUND_SIZES = (1, 1, 2, 4, 4, 4, 4, 4, 4, 4)
+ROUNDS = len(ROUND_SIZES)
+FIRST_PASS = [sum(ROUND_SIZES[:i]) for i in range(ROUNDS)]
+MAX_ROUND = max(ROUND_SIZES)
+X_BUFS = 5
+W_BUFS = 16
+H_LOAD_BEFORE_X_ROUND = 6
+H_ROUND = ROUNDS - 3
+H_PLANE_ROUND = 3
 
 FLOPS = 2 * BATCH * (IN_SIZE + HIDDEN) * GATES
 
@@ -41,13 +47,13 @@ def tile_layernormgrucell_pa_k_kernel(
         ctx.enter_context(tc.manual_schedule())
 
         const = ctx.enter_context(tc.tile_pool(name="const", bufs=1))
-        x_pool = ctx.enter_context(tc.tile_pool(name="x", bufs=W_ROUNDS_AHEAD + X_ROUNDS_AHEAD))
-        w_pool = ctx.enter_context(tc.tile_pool(name="w", bufs=(W_ROUNDS_AHEAD + 1) * ROUND))
+        x_pool = ctx.enter_context(tc.tile_pool(name="x", bufs=X_BUFS))
+        w_pool = ctx.enter_context(tc.tile_pool(name="w", bufs=W_BUFS))
         quant_pool = ctx.enter_context(tc.tile_pool(name="quant", bufs=2))
         rows_pool = ctx.enter_context(tc.tile_pool(name="rows", bufs=ROW_TILES))
         stat_pool = ctx.enter_context(tc.tile_pool(name="stat", bufs=2 * ROW_TILES))
         sum_banks = ctx.enter_context(tc.psum_pool(name="sums", bufs=1))
-        spare_banks = ctx.enter_context(tc.psum_pool(name="spare", bufs=ROUND))
+        spare_banks = ctx.enter_context(tc.psum_pool(name="spare", bufs=4))
 
         x_rows = x.rearrange("(m p) k -> p m k", p=P)
         h_rows = h.rearrange("(m p) k -> p m k", p=P)
@@ -60,68 +66,79 @@ def tile_layernormgrucell_pa_k_kernel(
         def col_tile(n):
             return slice(n * N_TILE, (n + 1) * N_TILE)
 
-        w_planes = const.tile([P, ROUNDS + 1, GATES], U8, align_bytes=64)
-        nc.vector.memset(w_planes[:].rearrange("p r n -> p (r n)").bitcast(I32), 0)
+        w_planes = const.tile([P, PLANE_GROUPS + 1, GATES], U8, align_bytes=64)
+        nc.vector.memset(w_planes[:, 0, :].bitcast(I32), 0)
         bias_rows = const.tile([P, 2 * GATES], BF16)
         nc.vector.memset(bias_rows[:].bitcast(I32), 0)
         ones = const.tile([P, P], BF16)
         nc.vector.memset(ones[:], 1.0)
         neg_half = const.tile([P, ROW_TILES], F32)
         nc.vector.memset(neg_half[:], -0.5)
+        nc.vector.memset(w_planes[:, 1:, :].rearrange("p r n -> p (r n)").bitcast(I32), 0)
         identity = const.tile([P, P], F32)
         make_identity(nc, identity[:])
 
-        def load_x(r):
-            x_sb = x_pool.tile([P, ROW_TILES, ROUND * K_PASS], BF16, name="x_sb")
-            k_cols = slice(r * ROUND * K_PASS, (r + 1) * ROUND * K_PASS)
+        x_tiles = {}
+        w_tiles = {}
+        h_sb = const.tile([P, ROW_TILES, HIDDEN], BF16)
+        wh_sb = const.tile([P, GATES], U32, align_bytes=64)
+
+        def load_x(i):
+            x_sb = x_pool.tile([P, ROW_TILES, ROUND_SIZES[i] * K_PASS], BF16, name="x_sb")
+            k_cols = slice(FIRST_PASS[i] * K_PASS, (FIRST_PASS[i] + ROUND_SIZES[i]) * K_PASS)
             nc.sync.dma_start(out=x_sb[:], in_=x_rows[:, :, k_cols])
-            return x_sb
+            x_tiles[i] = x_sb
 
         def load_w(g):
             w_sb = w_pool.tile([P, GATES], U32, name="w_sb", align_bytes=64)
             nc.sync.dma_start(out=w_sb[:].bitcast(I32), in_=wi_words[g])
-            return w_sb
+            w_tiles[g] = w_sb
 
-        def load_scale_planes(r):
+        def load_h(unused):
+            nc.sync.dma_start(out=h_sb[:], in_=h_rows)
+            nc.sync.dma_start(out=wh_sb[:].bitcast(I32), in_=wh_words[0])
+
+        def load_scale_planes(engine, r):
             for quadrant in range(4):
-                nc.gpsimd.dma_start(
+                engine.dma_start(
                     out=w_planes[32 * quadrant : 32 * quadrant + 16, r, :].bitcast(F32),
-                    in_=wi_scales[r * ROUND : (r + 1) * ROUND, 4 * quadrant : 4 * quadrant + 4, :],
+                    in_=wi_scales[
+                        r * PLANE_GROUP : (r + 1) * PLANE_GROUP, 4 * quadrant : 4 * quadrant + 4, :
+                    ],
                 )
 
-        x_tiles = {}
-        w_tiles = {}
+        queue = [("x", 0), ("x", 1)]
+        for i in range(ROUNDS):
+            if i + 2 < ROUNDS:
+                if i + 2 == H_LOAD_BEFORE_X_ROUND:
+                    queue.append(("h", 0))
+                queue.append(("x", i + 2))
+            for g in range(FIRST_PASS[i], FIRST_PASS[i] + ROUND_SIZES[i]):
+                queue.append(("w", g))
+        loaders = {"x": load_x, "w": load_w, "h": load_h}
 
-        def load_round(r):
-            if r + X_ROUNDS_AHEAD < ROUNDS:
-                x_tiles[r + X_ROUNDS_AHEAD] = load_x(r + X_ROUNDS_AHEAD)
-            for g in range(r * ROUND, (r + 1) * ROUND):
-                w_tiles[g] = load_w(g)
+        issued = {"count": 0}
 
-        h_sb = const.tile([P, ROW_TILES, HIDDEN], BF16)
-        nc.sync.dma_start(out=h_sb[:], in_=h_rows)
-        wh_sb = const.tile([P, GATES], U32, align_bytes=64)
-        nc.sync.dma_start(out=wh_sb[:].bitcast(I32), in_=wh_words[0])
-        for r in range(X_ROUNDS_AHEAD):
-            x_tiles[r] = load_x(r)
-        for r in range(W_ROUNDS_AHEAD):
-            load_round(r)
+        def issue_loads(sorted_rounds, multiplied_passes):
+            for kind, index in queue[issued["count"] :]:
+                if kind == "x" and index >= X_BUFS + sorted_rounds:
+                    break
+                if kind == "w" and index >= W_BUFS + multiplied_passes:
+                    break
+                loaders[kind](index)
+                issued["count"] += 1
 
         nc.scalar.dma_start(out=bias_rows[0:1, 0:GATES], in_=b_irz.unsqueeze(0))
         nc.scalar.dma_start(out=bias_rows[0:1, GATES : 2 * GATES], in_=b_hrz.unsqueeze(0))
-        for quadrant in range(4):
-            nc.scalar.dma_start(
-                out=w_planes[32 * quadrant : 32 * quadrant + 4, ROUNDS, :].bitcast(F32),
-                in_=wh_scales[0, 4 * quadrant : 4 * quadrant + 4, :],
-            )
-        for r in range(PLANE_ROUNDS_FIRST):
-            load_scale_planes(r)
+        load_scale_planes(nc.scalar, 0)
+        for r in range(1, PLANE_GROUPS):
+            load_scale_planes(nc.gpsimd, r)
 
         table_warmer = const.tile([P, 1], F32)
         nc.scalar.activation(out=table_warmer[:], in_=neg_half[:, 0:1], func=ACT.Sigmoid)
 
-        def sort_words(rows_sb, passes, label):
-            sorted_words = quant_pool.tile(
+        def sort_words(pool, rows_sb, passes, label):
+            sorted_words = pool.tile(
                 [P, ROW_TILES * passes, 2, P], F32, name=label + "_sorted_words"
             )
             nc.vector.tensor_copy(
@@ -130,8 +147,8 @@ def tile_layernormgrucell_pa_k_kernel(
             )
             return sorted_words
 
-        def transpose_and_quantise(sorted_words, passes, label):
-            grouped = quant_pool.tile(
+        def turn(pool, sorted_words, passes, label):
+            grouped = pool.tile(
                 [P, passes * BATCH * PACK], BF16, name=label + "_grouped", align_bytes=64
             )
             grouped_words = grouped[:].bitcast(F32).rearrange("p (g c u) -> p g c u", g=passes, u=2)
@@ -145,19 +162,13 @@ def tile_layernormgrucell_pa_k_kernel(
                             identity[:],
                         )
                 nc.scalar.copy(out=grouped_words[:, g], in_=turned[:].rearrange("p u c -> p c u"))
-            codes = quant_pool.tile([P, passes * BATCH], U32, name=label + "_codes", align_bytes=64)
-            scales = quant_pool.tile([P, passes * BATCH], U8, name=label + "_scales", align_bytes=64)
+            return grouped
+
+        def quantise(pool, grouped, passes, label):
+            codes = pool.tile([P, passes * BATCH], U32, name=label + "_codes", align_bytes=64)
+            scales = pool.tile([P, passes * BATCH], U8, name=label + "_scales", align_bytes=64)
             nc.vector.quantize_mx(out=codes[:].bitcast(FP8X4), scales=scales[:], in_=grouped[:])
             return codes, scales
-
-        def new_sums():
-            return [
-                [
-                    sum_banks.tile([P, N_TILE], F32, name="sums_%d_%d" % (m, n))
-                    for n in range(COL_TILES)
-                ]
-                for m in range(ROW_TILES)
-            ]
 
         def multiply(sums, quantised, g_local, n, w_sb, plane, first, last):
             codes, scales = quantised
@@ -209,7 +220,11 @@ def tile_layernormgrucell_pa_k_kernel(
             )
             return rstd, shift
 
-        h_quantised = transpose_and_quantise(sort_words(h_sb, 1, "h"), 1, "h")
+        issue_loads(0, 0)
+
+        x_sorted = {i: sort_words(quant_pool, x_tiles[i], ROUND_SIZES[i], "x") for i in range(2)}
+        x_grouped = {i: turn(quant_pool, x_sorted[i], ROUND_SIZES[i], "x") for i in range(2)}
+        x_quantised = {0: quantise(quant_pool, x_grouped[0], ROUND_SIZES[0], "x")}
 
         bias = const.tile([P, 2 * GATES], F32)
         for c in range(2 * COL_TILES):
@@ -221,49 +236,72 @@ def tile_layernormgrucell_pa_k_kernel(
         x_bias = bias[:, 0:GATES]
         h_bias = bias[:, GATES : 2 * GATES]
 
-        h_sums = new_sums()
-        for n in range(COL_TILES):
-            multiply(h_sums, h_quantised, 0, n, wh_sb, w_planes[:, ROUNDS, :], True, True)
+        x_sums = [
+            [sum_banks.tile([P, N_TILE], F32, name="sums_%d_%d" % (m, n)) for n in range(COL_TILES)]
+            for m in range(ROW_TILES)
+        ]
+        h_state = {}
+        for i in range(ROUNDS):
+            size = ROUND_SIZES[i]
+            issue_loads(i + 2, FIRST_PASS[i])
+            if i == H_PLANE_ROUND:
+                for quadrant in range(4):
+                    nc.scalar.dma_start(
+                        out=w_planes[32 * quadrant : 32 * quadrant + 4, PLANE_GROUPS, :].bitcast(F32),
+                        in_=wh_scales[0, 4 * quadrant : 4 * quadrant + 4, :],
+                    )
+            if i + 2 < ROUNDS:
+                x_sorted[i + 2] = sort_words(quant_pool, x_tiles[i + 2], ROUND_SIZES[i + 2], "x")
+            if i == H_ROUND - 2:
+                h_state["sorted"] = sort_words(const, h_sb, 1, "h")
+            if 0 < i and i + 1 < ROUNDS:
+                x_grouped[i + 1] = turn(quant_pool, x_sorted[i + 1], ROUND_SIZES[i + 1], "x")
+            if i == H_ROUND - 1:
+                h_state["grouped"] = turn(const, h_state["sorted"], 1, "h")
+            if i + 1 < ROUNDS:
+                x_quantised[i + 1] = quantise(quant_pool, x_grouped[i + 1], ROUND_SIZES[i + 1], "x")
+            if i == H_ROUND - 1:
+                h_state["quantised"] = quantise(const, h_state["grouped"], 1, "h")
 
-        x_sorted = {0: sort_words(x_tiles[0], ROUND, "x")}
-        h_v = new_rows("v")
-        for n in range(COL_TILES):
-            add_bias(h_v, h_sums, h_bias, n)
-        x_sorted[1] = sort_words(x_tiles[1], ROUND, "x")
-        x_quantised = {0: transpose_and_quantise(x_sorted[0], ROUND, "x")}
-
-        h_stats = new_stats()
-        for n in range(COL_TILES):
-            measure(h_stats, h_v, n)
-        h_norm = new_rows("h_norm")
-        h_rstd, h_shift = scale_and_shift(h_stats)
-        for m in range(ROW_TILES):
-            nc.vector.tensor_scalar(
-                out=h_norm[m][:], in0=h_v[m][:],
-                scalar1=h_rstd[:, m : m + 1], scalar2=h_shift[:, m : m + 1],
-                op0=ALU.mult, op1=ALU.add,
-            )
-        for r in range(PLANE_ROUNDS_FIRST, ROUNDS):
-            load_scale_planes(r)
-
-        x_sums = new_sums()
-        for r in range(ROUNDS):
-            if r + W_ROUNDS_AHEAD < ROUNDS:
-                load_round(r + W_ROUNDS_AHEAD)
-            if r + 2 < ROUNDS:
-                x_sorted[r + 2] = sort_words(x_tiles[r + 2], ROUND, "x")
-            if r + 1 < ROUNDS:
-                x_quantised[r + 1] = transpose_and_quantise(x_sorted[r + 1], ROUND, "x")
-            if r + 1 < ROUNDS:
-                steps = [(j, n) for j in range(ROUND) for n in range(COL_TILES)]
+            if i + 1 < ROUNDS:
+                steps = [(j, n) for j in range(size) for n in range(COL_TILES)]
             else:
-                steps = [(j, n) for n in range(COL_TILES) for j in range(ROUND)]
-            for j, n in steps:
-                g = r * ROUND + j
+                steps = [(j, n) for n in range(COL_TILES) for j in range(size)]
+            for s, (j, n) in enumerate(steps):
+                if i == H_ROUND and s == len(steps) // 2:
+                    h_sums = [
+                        [
+                            spare_banks.tile([P, N_TILE], F32, name="h_sums", tag="spare")
+                            for nn in range(COL_TILES)
+                        ]
+                        for m in range(ROW_TILES)
+                    ]
+                    for nn in range(COL_TILES):
+                        multiply(
+                            h_sums, h_state["quantised"], 0, nn, wh_sb,
+                            w_planes[:, PLANE_GROUPS, :], True, True,
+                        )
+                g = FIRST_PASS[i] + j
                 multiply(
-                    x_sums, x_quantised[r], j, n, w_tiles[g], w_planes[4 * j : P, r, :],
+                    x_sums, x_quantised[i], j, n, w_tiles[g],
+                    w_planes[4 * (g % PLANE_GROUP) : P, g // PLANE_GROUP, :],
                     g == 0, g == X_PASSES - 1,
                 )
+            if i == H_ROUND:
+                h_v = new_rows("v")
+                h_stats = new_stats()
+                for n in range(COL_TILES):
+                    add_bias(h_v, h_sums, h_bias, n)
+                for n in range(COL_TILES):
+                    measure(h_stats, h_v, n)
+                h_norm = new_rows("h_norm")
+                h_rstd, h_shift = scale_and_shift(h_stats)
+                for m in range(ROW_TILES):
+                    nc.vector.tensor_scalar(
+                        out=h_norm[m][:], in0=h_v[m][:],
+                        scalar1=h_rstd[:, m : m + 1], scalar2=h_shift[:, m : m + 1],
+                        op0=ALU.mult, op1=ALU.add,
+                    )
 
         x_v = new_rows("v")
         x_stats = new_stats()

@@ -30,7 +30,7 @@ ROUND_SIZES = (1, 1, 2, 4, 4, 4, 4, 4, 4, 4)
 ROUNDS = len(ROUND_SIZES)
 FIRST_PASS = [sum(ROUND_SIZES[:i]) for i in range(ROUNDS)]
 MAX_ROUND = max(ROUND_SIZES)
-X_BUFS = 5
+X_BUFS = 4
 W_BUFS = 16
 H_LOAD_BEFORE_X_ROUND = 6
 H_ROUND = ROUNDS - 3
@@ -49,6 +49,9 @@ def tile_layernormgrucell_pa_k_kernel(
         const = ctx.enter_context(tc.tile_pool(name="const", bufs=1))
         x_pool = ctx.enter_context(tc.tile_pool(name="x", bufs=X_BUFS))
         w_pool = ctx.enter_context(tc.tile_pool(name="w", bufs=W_BUFS))
+        w_last_pool = ctx.enter_context(
+            tc.tile_pool(name="w_last", bufs=COL_TILES * ROUND_SIZES[-1])
+        )
         quant_pool = ctx.enter_context(tc.tile_pool(name="quant", bufs=2))
         rows_pool = ctx.enter_context(tc.tile_pool(name="rows", bufs=ROW_TILES))
         stat_pool = ctx.enter_context(tc.tile_pool(name="stat", bufs=2 * ROW_TILES))
@@ -80,6 +83,7 @@ def tile_layernormgrucell_pa_k_kernel(
 
         x_tiles = {}
         w_tiles = {}
+        w_halves = {}
         h_sb = const.tile([P, ROW_TILES, HIDDEN], BF16)
         wh_sb = const.tile([P, GATES], U32, align_bytes=64)
 
@@ -93,6 +97,12 @@ def tile_layernormgrucell_pa_k_kernel(
             w_sb = w_pool.tile([P, GATES], U32, name="w_sb", align_bytes=64)
             nc.sync.dma_start(out=w_sb[:].bitcast(I32), in_=wi_words[g])
             w_tiles[g] = w_sb
+
+        def load_w_half(g_n):
+            g, n = g_n
+            w_half = w_last_pool.tile([P, N_TILE], U32, name="w_half", align_bytes=64)
+            nc.sync.dma_start(out=w_half[:].bitcast(I32), in_=wi_words[g][:, col_tile(n)])
+            w_halves[g_n] = w_half
 
         def load_h(unused):
             nc.sync.dma_start(out=h_sb[:], in_=h_rows)
@@ -113,9 +123,12 @@ def tile_layernormgrucell_pa_k_kernel(
                 if i + 2 == H_LOAD_BEFORE_X_ROUND:
                     queue.append(("h", 0))
                 queue.append(("x", i + 2))
-            for g in range(FIRST_PASS[i], FIRST_PASS[i] + ROUND_SIZES[i]):
-                queue.append(("w", g))
-        loaders = {"x": load_x, "w": load_w, "h": load_h}
+            passes = range(FIRST_PASS[i], FIRST_PASS[i] + ROUND_SIZES[i])
+            if i + 1 < ROUNDS:
+                queue.extend([("w", g) for g in passes])
+            else:
+                queue.extend([("half", (g, n)) for n in range(COL_TILES) for g in passes])
+        loaders = {"x": load_x, "w": load_w, "half": load_w_half, "h": load_h}
 
         issued = {"count": 0}
 
@@ -170,19 +183,18 @@ def tile_layernormgrucell_pa_k_kernel(
             nc.vector.quantize_mx(out=codes[:].bitcast(FP8X4), scales=scales[:], in_=grouped[:])
             return codes, scales
 
-        def multiply(sums, quantised, g_local, n, w_sb, plane, first, last):
+        def multiply(bank, quantised, j, m, w_cols, plane_cols, first, last):
             codes, scales = quantised
-            for m in range(ROW_TILES):
-                rows = slice(g_local * BATCH + m * P, g_local * BATCH + (m + 1) * P)
-                nc.tensor.matmul_mx(
-                    out=sums[m][n][:],
-                    lhsT=codes[:, rows].bitcast(FP8X4),
-                    lhsT_scale=scales[:, rows],
-                    rhs=w_sb[:, col_tile(n)].bitcast(FP8X4),
-                    rhs_scale=plane[:, col_tile(n)],
-                    start=first,
-                    stop=last,
-                )
+            rows = slice(j * BATCH + m * P, j * BATCH + (m + 1) * P)
+            nc.tensor.matmul_mx(
+                out=bank[:],
+                lhsT=codes[:, rows].bitcast(FP8X4),
+                lhsT_scale=scales[:, rows],
+                rhs=w_cols.bitcast(FP8X4),
+                rhs_scale=plane_cols,
+                start=first,
+                stop=last,
+            )
 
         def new_rows(label):
             return [rows_pool.tile([P, GATES], F32, name=label) for m in range(ROW_TILES)]
@@ -192,16 +204,14 @@ def tile_layernormgrucell_pa_k_kernel(
                 stat_pool.tile([P, COL_TILES, 6], F32, name="stats") for m in range(ROW_TILES)
             ]
 
-        def add_bias(v, sums, bias_cols, n):
-            for m in range(ROW_TILES):
-                nc.vector.tensor_tensor(
-                    out=v[m][:, col_tile(n)], in0=sums[m][n][:], in1=bias_cols[:, col_tile(n)],
-                    op=ALU.add,
-                )
+        def add_bias(v, sums, bias_cols, m, n):
+            nc.vector.tensor_tensor(
+                out=v[m][:, col_tile(n)], in0=sums[m][n][:], in1=bias_cols[:, col_tile(n)],
+                op=ALU.add,
+            )
 
-        def measure(stats, v, n):
-            for m in range(ROW_TILES):
-                nc.vector.bn_stats(out=stats[m][:, n, :], in_=v[m][:, col_tile(n)])
+        def measure(stats, v, m, n):
+            nc.vector.bn_stats(out=stats[m][:, n, :], in_=v[m][:, col_tile(n)])
 
         def scale_and_shift(stats):
             mean_var = stat_pool.tile([P, ROW_TILES, 2], F32, name="mean_var")
@@ -264,10 +274,16 @@ def tile_layernormgrucell_pa_k_kernel(
                 h_state["quantised"] = quantise(const, h_state["grouped"], 1, "h")
 
             if i + 1 < ROUNDS:
-                steps = [(j, n) for j in range(size) for n in range(COL_TILES)]
+                steps = [
+                    (j, m, n)
+                    for j in range(size) for n in range(COL_TILES) for m in range(ROW_TILES)
+                ]
             else:
-                steps = [(j, n) for n in range(COL_TILES) for j in range(size)]
-            for s, (j, n) in enumerate(steps):
+                steps = [
+                    (j, m, n)
+                    for n in range(COL_TILES) for m in range(ROW_TILES) for j in range(size)
+                ]
+            for s, (j, m, n) in enumerate(steps):
                 if i == H_ROUND and s == len(steps) // 2:
                     h_sums = [
                         [
@@ -277,23 +293,28 @@ def tile_layernormgrucell_pa_k_kernel(
                         for m in range(ROW_TILES)
                     ]
                     for nn in range(COL_TILES):
-                        multiply(
-                            h_sums, h_state["quantised"], 0, nn, wh_sb,
-                            w_planes[:, PLANE_GROUPS, :], True, True,
-                        )
+                        for mm in range(ROW_TILES):
+                            multiply(
+                                h_sums[mm][nn], h_state["quantised"], 0, mm,
+                                wh_sb[:, col_tile(nn)], w_planes[:, PLANE_GROUPS, col_tile(nn)],
+                                True, True,
+                            )
                 g = FIRST_PASS[i] + j
                 multiply(
-                    x_sums, x_quantised[i], j, n, w_tiles[g],
-                    w_planes[4 * (g % PLANE_GROUP) : P, g // PLANE_GROUP, :],
+                    x_sums[m][n], x_quantised[i], j, m,
+                    w_tiles[g][:, col_tile(n)] if i + 1 < ROUNDS else w_halves[(g, n)][:],
+                    w_planes[4 * (g % PLANE_GROUP) : P, g // PLANE_GROUP, col_tile(n)],
                     g == 0, g == X_PASSES - 1,
                 )
             if i == H_ROUND:
                 h_v = new_rows("v")
                 h_stats = new_stats()
                 for n in range(COL_TILES):
-                    add_bias(h_v, h_sums, h_bias, n)
+                    for m in range(ROW_TILES):
+                        add_bias(h_v, h_sums, h_bias, m, n)
                 for n in range(COL_TILES):
-                    measure(h_stats, h_v, n)
+                    for m in range(ROW_TILES):
+                        measure(h_stats, h_v, m, n)
                 h_norm = new_rows("h_norm")
                 h_rstd, h_shift = scale_and_shift(h_stats)
                 for m in range(ROW_TILES):
@@ -306,8 +327,9 @@ def tile_layernormgrucell_pa_k_kernel(
         x_v = new_rows("v")
         x_stats = new_stats()
         for n in range(COL_TILES):
-            add_bias(x_v, x_sums, x_bias, n)
-            measure(x_stats, x_v, n)
+            for m in range(ROW_TILES):
+                add_bias(x_v, x_sums, x_bias, m, n)
+                measure(x_stats, x_v, m, n)
         x_rstd, x_shift = scale_and_shift(x_stats)
         z = new_rows("z")
         gates = new_rows("gates")

@@ -32,9 +32,11 @@ FIRST_PASS = [sum(ROUND_SIZES[:i]) for i in range(ROUNDS)]
 MAX_ROUND = max(ROUND_SIZES)
 X_BUFS = 4
 W_BUFS = 16
-H_LOAD_BEFORE_X_ROUND = 6
-H_ROUND = ROUNDS - 3
-H_PLANE_ROUND = 3
+H_LOAD_BEFORE_X_ROUND = 5
+H_ROUND = 4
+H_PLANE_ROUND = 1
+H_NORM_ROUND = ROUNDS - 2
+T_LEAD = 2
 
 FLOPS = 2 * BATCH * (IN_SIZE + HIDDEN) * GATES
 
@@ -53,6 +55,7 @@ def tile_layernormgrucell_pa_k_kernel(
             tc.tile_pool(name="w_last", bufs=COL_TILES * ROUND_SIZES[-1])
         )
         quant_pool = ctx.enter_context(tc.tile_pool(name="quant", bufs=2))
+        codes_pool = ctx.enter_context(tc.tile_pool(name="codes", bufs=T_LEAD + 1))
         rows_pool = ctx.enter_context(tc.tile_pool(name="rows", bufs=ROW_TILES))
         stat_pool = ctx.enter_context(tc.tile_pool(name="stat", bufs=2 * ROW_TILES))
         sum_banks = ctx.enter_context(tc.psum_pool(name="sums", bufs=1))
@@ -117,12 +120,12 @@ def tile_layernormgrucell_pa_k_kernel(
                     ],
                 )
 
-        queue = [("x", 0), ("x", 1)]
+        queue = [("x", i) for i in range(T_LEAD + 1)]
         for i in range(ROUNDS):
-            if i + 2 < ROUNDS:
-                if i + 2 == H_LOAD_BEFORE_X_ROUND:
+            if i + T_LEAD + 1 < ROUNDS:
+                if i + T_LEAD + 1 == H_LOAD_BEFORE_X_ROUND:
                     queue.append(("h", 0))
-                queue.append(("x", i + 2))
+                queue.append(("x", i + T_LEAD + 1))
             passes = range(FIRST_PASS[i], FIRST_PASS[i] + ROUND_SIZES[i])
             if i + 1 < ROUNDS:
                 queue.extend([("w", g) for g in passes])
@@ -213,7 +216,7 @@ def tile_layernormgrucell_pa_k_kernel(
         def measure(stats, v, m, n):
             nc.vector.bn_stats(out=stats[m][:, n, :], in_=v[m][:, col_tile(n)])
 
-        def scale_and_shift(stats):
+        def mean_and_rstd(stats):
             mean_var = stat_pool.tile([P, ROW_TILES, 2], F32, name="mean_var")
             for m in range(ROW_TILES):
                 nc.vector.bn_aggr(
@@ -223,18 +226,23 @@ def tile_layernormgrucell_pa_k_kernel(
             nc.vector.tensor_scalar_add(var_eps[:], mean_var[:, :, 1], EPS)
             rstd = stat_pool.tile([P, ROW_TILES], F32, name="rstd")
             nc.gpsimd.tensor_tensor(out=rstd[:], in0=var_eps[:], in1=neg_half[:], op=ALU.pow)
+            return mean_var, rstd
+
+        def shift_of(mean_var, rstd):
             shift = stat_pool.tile([P, ROW_TILES], F32, name="shift")
             nc.vector.scalar_tensor_tensor(
                 out=shift[:], in0=mean_var[:, :, 0], scalar=-1.0, in1=rstd[:],
                 op0=ALU.mult, op1=ALU.mult,
             )
-            return rstd, shift
+            return shift
 
         issue_loads(0, 0)
 
         x_sorted = {i: sort_words(quant_pool, x_tiles[i], ROUND_SIZES[i], "x") for i in range(2)}
         x_grouped = {i: turn(quant_pool, x_sorted[i], ROUND_SIZES[i], "x") for i in range(2)}
-        x_quantised = {0: quantise(quant_pool, x_grouped[0], ROUND_SIZES[0], "x")}
+        x_quantised = {0: quantise(codes_pool, x_grouped[0], ROUND_SIZES[0], "x")}
+        x_sorted[2] = sort_words(quant_pool, x_tiles[2], ROUND_SIZES[2], "x")
+        x_quantised[1] = quantise(codes_pool, x_grouped[1], ROUND_SIZES[1], "x")
 
         bias = const.tile([P, 2 * GATES], F32)
         for c in range(2 * COL_TILES):
@@ -253,23 +261,26 @@ def tile_layernormgrucell_pa_k_kernel(
         h_state = {}
         for i in range(ROUNDS):
             size = ROUND_SIZES[i]
-            issue_loads(i + 2, FIRST_PASS[i])
+            issue_loads(i + T_LEAD + 1, FIRST_PASS[i])
             if i == H_PLANE_ROUND:
                 for quadrant in range(4):
                     nc.scalar.dma_start(
                         out=w_planes[32 * quadrant : 32 * quadrant + 4, PLANE_GROUPS, :].bitcast(F32),
                         in_=wh_scales[0, 4 * quadrant : 4 * quadrant + 4, :],
                     )
-            if i + 2 < ROUNDS:
-                x_sorted[i + 2] = sort_words(quant_pool, x_tiles[i + 2], ROUND_SIZES[i + 2], "x")
+            ahead = i + T_LEAD
+            if ahead + 1 < ROUNDS:
+                x_sorted[ahead + 1] = sort_words(
+                    quant_pool, x_tiles[ahead + 1], ROUND_SIZES[ahead + 1], "x"
+                )
             if i == H_ROUND - 2:
                 h_state["sorted"] = sort_words(const, h_sb, 1, "h")
-            if 0 < i and i + 1 < ROUNDS:
-                x_grouped[i + 1] = turn(quant_pool, x_sorted[i + 1], ROUND_SIZES[i + 1], "x")
+            if ahead < ROUNDS:
+                x_grouped[ahead] = turn(quant_pool, x_sorted[ahead], ROUND_SIZES[ahead], "x")
             if i == H_ROUND - 1:
                 h_state["grouped"] = turn(const, h_state["sorted"], 1, "h")
-            if i + 1 < ROUNDS:
-                x_quantised[i + 1] = quantise(quant_pool, x_grouped[i + 1], ROUND_SIZES[i + 1], "x")
+            if ahead < ROUNDS:
+                x_quantised[ahead] = quantise(codes_pool, x_grouped[ahead], ROUND_SIZES[ahead], "x")
             if i == H_ROUND - 1:
                 h_state["quantised"] = quantise(const, h_state["grouped"], 1, "h")
 
@@ -315,8 +326,10 @@ def tile_layernormgrucell_pa_k_kernel(
                 for n in range(COL_TILES):
                     for m in range(ROW_TILES):
                         measure(h_stats, h_v, m, n)
+                h_mean_var, h_rstd = mean_and_rstd(h_stats)
+            if i == H_NORM_ROUND:
                 h_norm = new_rows("h_norm")
-                h_rstd, h_shift = scale_and_shift(h_stats)
+                h_shift = shift_of(h_mean_var, h_rstd)
                 for m in range(ROW_TILES):
                     nc.vector.tensor_scalar(
                         out=h_norm[m][:], in0=h_v[m][:],
@@ -325,13 +338,56 @@ def tile_layernormgrucell_pa_k_kernel(
                     )
 
         x_v = new_rows("v")
-        x_stats = new_stats()
+        z = new_rows("z")
+        sum_v = stat_pool.tile([P, ROW_TILES, COL_TILES], F32, name="sum_v")
+        sum_sq = stat_pool.tile([P, ROW_TILES, COL_TILES], F32, name="sum_sq")
+        neg_pivot = stat_pool.tile([P, ROW_TILES], F32, name="neg_pivot")
+        first_part = stat_pool.tile([P, ROW_TILES], F32, name="first_part")
         for n in range(COL_TILES):
             for m in range(ROW_TILES):
-                add_bias(x_v, x_sums, x_bias, m, n)
-                measure(x_stats, x_v, m, n)
-        x_rstd, x_shift = scale_and_shift(x_stats)
-        z = new_rows("z")
+                cols = col_tile(n)
+                if (m, n) == (ROW_TILES - 1, COL_TILES - 1):
+                    nc.vector.tensor_scalar(
+                        out=first_part[:], in0=sum_sq[:, :, 0], scalar1=1.0 / GATES, scalar2=EPS,
+                        op0=ALU.mult, op1=ALU.add,
+                    )
+                nc.vector.scalar_tensor_tensor(
+                    out=x_v[m][:, cols], in0=x_sums[m][n][:], scalar=1.0, in1=x_bias[:, cols],
+                    op0=ALU.mult, op1=ALU.add, accum_out=sum_v[:, m, n : n + 1],
+                )
+                if n == 0:
+                    nc.vector.tensor_scalar_mul(
+                        neg_pivot[:, m : m + 1], sum_v[:, m, 0:1], -1.0 / N_TILE
+                    )
+                nc.scalar.activation(
+                    out=z[m][:, cols], in_=x_v[m][:, cols], func=ACT.Square,
+                    bias=neg_pivot[:, m : m + 1], accum_out=sum_sq[:, m, n : n + 1],
+                )
+        off_pivot = stat_pool.tile([P, ROW_TILES], F32, name="off_pivot")
+        nc.vector.tensor_tensor(
+            out=off_pivot[:], in0=sum_v[:, :, 1], in1=sum_v[:, :, 0], op=ALU.subtract
+        )
+        neg_square = stat_pool.tile([P, ROW_TILES], F32, name="neg_square")
+        nc.vector.scalar_tensor_tensor(
+            out=neg_square[:], in0=off_pivot[:], scalar=-1.0 / (GATES * GATES), in1=off_pivot[:],
+            op0=ALU.mult, op1=ALU.mult,
+        )
+        known_part = stat_pool.tile([P, ROW_TILES], F32, name="known_part")
+        nc.vector.tensor_tensor(
+            out=known_part[:], in0=first_part[:], in1=neg_square[:], op=ALU.add
+        )
+        x_var_eps = stat_pool.tile([P, ROW_TILES], F32, name="var_eps")
+        nc.vector.scalar_tensor_tensor(
+            out=x_var_eps[:], in0=sum_sq[:, :, 1], scalar=1.0 / GATES, in1=known_part[:],
+            op0=ALU.mult, op1=ALU.add,
+        )
+        x_rstd = stat_pool.tile([P, ROW_TILES], F32, name="rstd")
+        nc.gpsimd.tensor_tensor(out=x_rstd[:], in0=x_var_eps[:], in1=neg_half[:], op=ALU.pow)
+        row_sum = stat_pool.tile([P, ROW_TILES], F32, name="row_sum")
+        nc.vector.tensor_tensor(
+            out=row_sum[:], in0=sum_v[:, :, 0], in1=sum_v[:, :, 1], op=ALU.add
+        )
+        x_shift = stat_pool.tile([P, ROW_TILES], F32, name="shift")
         gates = new_rows("gates")
         for m in range(ROW_TILES):
             for n in range(COL_TILES):
@@ -340,6 +396,11 @@ def tile_layernormgrucell_pa_k_kernel(
                     out=z[m][:, cols], in0=x_v[m][:, cols], scalar=x_rstd[:, m : m + 1],
                     in1=h_norm[m][:, cols], op0=ALU.mult, op1=ALU.add,
                 )
+                if (m, n) == (0, 0):
+                    nc.vector.scalar_tensor_tensor(
+                        out=x_shift[:], in0=row_sum[:], scalar=-1.0 / GATES, in1=x_rstd[:],
+                        op0=ALU.mult, op1=ALU.mult,
+                    )
                 nc.scalar.activation(
                     out=gates[m][:, cols], in_=z[m][:, cols], func=ACT.Sigmoid,
                     bias=x_shift[:, m : m + 1],

@@ -343,6 +343,41 @@ def tile_layernormgrucell_pa_k_kernel(
         sum_sq = stat_pool.tile([P, ROW_TILES, COL_TILES], F32, name="sum_sq")
         neg_pivot = stat_pool.tile([P, ROW_TILES], F32, name="neg_pivot")
         first_part = stat_pool.tile([P, ROW_TILES], F32, name="first_part")
+        off_pivot = stat_pool.tile([P, ROW_TILES], F32, name="off_pivot")
+        neg_square = stat_pool.tile([P, ROW_TILES], F32, name="neg_square")
+        known_part = stat_pool.tile([P, ROW_TILES], F32, name="known_part")
+        x_var_eps = stat_pool.tile([P, ROW_TILES], F32, name="var_eps")
+        x_rstd = stat_pool.tile([P, ROW_TILES], F32, name="rstd")
+
+        def step_off_pivot(m):
+            nc.vector.tensor_tensor(
+                out=off_pivot[:, m : m + 1], in0=sum_v[:, m, 1:2], in1=sum_v[:, m, 0:1],
+                op=ALU.subtract,
+            )
+
+        def step_neg_square(m):
+            nc.vector.scalar_tensor_tensor(
+                out=neg_square[:, m : m + 1], in0=off_pivot[:, m : m + 1],
+                scalar=-1.0 / (GATES * GATES), in1=off_pivot[:, m : m + 1],
+                op0=ALU.mult, op1=ALU.mult,
+            )
+
+        def step_known_part(m):
+            nc.vector.tensor_tensor(
+                out=known_part[:, m : m + 1], in0=first_part[:, m : m + 1],
+                in1=neg_square[:, m : m + 1], op=ALU.add,
+            )
+
+        def step_rstd(m):
+            nc.vector.scalar_tensor_tensor(
+                out=x_var_eps[:, m : m + 1], in0=sum_sq[:, m, 1:2], scalar=1.0 / GATES,
+                in1=known_part[:, m : m + 1], op0=ALU.mult, op1=ALU.add,
+            )
+            nc.gpsimd.tensor_tensor(
+                out=x_rstd[:, m : m + 1], in0=x_var_eps[:, m : m + 1], in1=neg_half[:, m : m + 1],
+                op=ALU.pow,
+            )
+
         for n in range(COL_TILES):
             for m in range(ROW_TILES):
                 cols = col_tile(n)
@@ -351,6 +386,7 @@ def tile_layernormgrucell_pa_k_kernel(
                         out=first_part[:], in0=sum_sq[:, :, 0], scalar1=1.0 / GATES, scalar2=EPS,
                         op0=ALU.mult, op1=ALU.add,
                     )
+                    step_off_pivot(0)
                 nc.vector.scalar_tensor_tensor(
                     out=x_v[m][:, cols], in0=x_sums[m][n][:], scalar=1.0, in1=x_bias[:, cols],
                     op0=ALU.mult, op1=ALU.add, accum_out=sum_v[:, m, n : n + 1],
@@ -363,26 +399,13 @@ def tile_layernormgrucell_pa_k_kernel(
                     out=z[m][:, cols], in_=x_v[m][:, cols], func=ACT.Square,
                     bias=neg_pivot[:, m : m + 1], accum_out=sum_sq[:, m, n : n + 1],
                 )
-        off_pivot = stat_pool.tile([P, ROW_TILES], F32, name="off_pivot")
-        nc.vector.tensor_tensor(
-            out=off_pivot[:], in0=sum_v[:, :, 1], in1=sum_v[:, :, 0], op=ALU.subtract
-        )
-        neg_square = stat_pool.tile([P, ROW_TILES], F32, name="neg_square")
-        nc.vector.scalar_tensor_tensor(
-            out=neg_square[:], in0=off_pivot[:], scalar=-1.0 / (GATES * GATES), in1=off_pivot[:],
-            op0=ALU.mult, op1=ALU.mult,
-        )
-        known_part = stat_pool.tile([P, ROW_TILES], F32, name="known_part")
-        nc.vector.tensor_tensor(
-            out=known_part[:], in0=first_part[:], in1=neg_square[:], op=ALU.add
-        )
-        x_var_eps = stat_pool.tile([P, ROW_TILES], F32, name="var_eps")
-        nc.vector.scalar_tensor_tensor(
-            out=x_var_eps[:], in0=sum_sq[:, :, 1], scalar=1.0 / GATES, in1=known_part[:],
-            op0=ALU.mult, op1=ALU.add,
-        )
-        x_rstd = stat_pool.tile([P, ROW_TILES], F32, name="rstd")
-        nc.gpsimd.tensor_tensor(out=x_rstd[:], in0=x_var_eps[:], in1=neg_half[:], op=ALU.pow)
+        step_neg_square(0)
+        step_off_pivot(1)
+        step_known_part(0)
+        step_neg_square(1)
+        step_rstd(0)
+        step_known_part(1)
+        step_rstd(1)
         row_sum = stat_pool.tile([P, ROW_TILES], F32, name="row_sum")
         nc.vector.tensor_tensor(
             out=row_sum[:], in0=sum_v[:, :, 0], in1=sum_v[:, :, 1], op=ALU.add
@@ -396,10 +419,10 @@ def tile_layernormgrucell_pa_k_kernel(
                     out=z[m][:, cols], in0=x_v[m][:, cols], scalar=x_rstd[:, m : m + 1],
                     in1=h_norm[m][:, cols], op0=ALU.mult, op1=ALU.add,
                 )
-                if (m, n) == (0, 0):
+                if n == 0:
                     nc.vector.scalar_tensor_tensor(
-                        out=x_shift[:], in0=row_sum[:], scalar=-1.0 / GATES, in1=x_rstd[:],
-                        op0=ALU.mult, op1=ALU.mult,
+                        out=x_shift[:, m : m + 1], in0=row_sum[:, m : m + 1], scalar=-1.0 / GATES,
+                        in1=x_rstd[:, m : m + 1], op0=ALU.mult, op1=ALU.mult,
                     )
                 nc.scalar.activation(
                     out=gates[m][:, cols], in_=z[m][:, cols], func=ACT.Sigmoid,

@@ -122,11 +122,15 @@ def tile_layernormgrucell_pa_k_kernel(
 
         queue = [("x", i) for i in range(T_LEAD + 1)]
         for i in range(ROUNDS):
+            passes = range(FIRST_PASS[i], FIRST_PASS[i] + ROUND_SIZES[i])
+            if ROUND_SIZES[i] < MAX_ROUND:
+                queue.extend([("w", g) for g in passes])
             if i + T_LEAD + 1 < ROUNDS:
                 if i + T_LEAD + 1 == H_LOAD_BEFORE_X_ROUND:
                     queue.append(("h", 0))
                 queue.append(("x", i + T_LEAD + 1))
-            passes = range(FIRST_PASS[i], FIRST_PASS[i] + ROUND_SIZES[i])
+            if ROUND_SIZES[i] < MAX_ROUND:
+                continue
             if i + 1 < ROUNDS:
                 queue.extend([("w", g) for g in passes])
             else:

from contextlib import ExitStack

import concourse.mybir as mybir
from concourse.masks import make_identity

F32 = mybir.dt.float32
BF16 = mybir.dt.bfloat16
I32 = mybir.dt.int32
U32 = mybir.dt.uint32
U8 = mybir.dt.uint8
FP8X4 = mybir.dt.float8_e4m3fn_x4
ALU = mybir.AluOpType
ACT = mybir.ActivationFunctionType

BATCH, IN_SIZE, HIDDEN = 256, 16384, 512
GATES = 2 * HIDDEN
EPS = 1e-5

P = 128
PACK = 4
K_PASS = P * PACK
N_TILE = 512
ROW_TILES = BATCH // P
COL_TILES = GATES // N_TILE
X_PASSES = IN_SIZE // K_PASS
PLANE_GROUP = 4
PLANE_GROUPS = X_PASSES // PLANE_GROUP

ROUND_SIZES = (1, 1, 2, 4, 4, 4, 4, 4, 4, 4)
ROUNDS = len(ROUND_SIZES)
FIRST_PASS = [sum(ROUND_SIZES[:i]) for i in range(ROUNDS)]
MAX_ROUND = max(ROUND_SIZES)
X_BUFS = 4
W_BUFS = 16
H_LOAD_BEFORE_X_ROUND = 5
H_ROUND = 4
H_PLANE_ROUND = 1
H_NORM_ROUND = ROUNDS - 2
T_LEAD = 2

FLOPS = 2 * BATCH * (IN_SIZE + HIDDEN) * GATES


def tile_layernormgrucell_pa_k_kernel(
    tc, x, h, w_irz_words, w_irz_scales, b_irz, w_hrz_words, w_hrz_scales, b_hrz, out
):
    nc = tc.nc
    with ExitStack() as ctx:
        ctx.enter_context(tc.manual_schedule())

        const = ctx.enter_context(tc.tile_pool(name="const", bufs=1))
        x_pool = ctx.enter_context(tc.tile_pool(name="x", bufs=X_BUFS))
        w_pool = ctx.enter_context(tc.tile_pool(name="w", bufs=W_BUFS))
        w_last_pool = ctx.enter_context(
            tc.tile_pool(name="w_last", bufs=COL_TILES * ROUND_SIZES[-1])
        )
        quant_pool = ctx.enter_context(tc.tile_pool(name="quant", bufs=2))
        codes_pool = ctx.enter_context(tc.tile_pool(name="codes", bufs=T_LEAD + 1))
        rows_pool = ctx.enter_context(tc.tile_pool(name="rows", bufs=ROW_TILES))
        stat_pool = ctx.enter_context(tc.tile_pool(name="stat", bufs=2 * ROW_TILES))
        sum_banks = ctx.enter_context(tc.psum_pool(name="sums", bufs=1))
        spare_banks = ctx.enter_context(tc.psum_pool(name="spare", bufs=4))

        x_rows = x.rearrange("(m p) k -> p m k", p=P)
        h_rows = h.rearrange("(m p) k -> p m k", p=P)
        out_rows = out.rearrange("(m p) n -> p m n", p=P)
        wi_words = w_irz_words.rearrange("g p n t -> g p (n t)").bitcast(I32)
        wh_words = w_hrz_words.rearrange("g p n t -> g p (n t)").bitcast(I32)
        wi_scales = w_irz_scales.bitcast(F32)
        wh_scales = w_hrz_scales.bitcast(F32)

        def col_tile(n):
            return slice(n * N_TILE, (n + 1) * N_TILE)

        w_planes = const.tile([P, PLANE_GROUPS + 1, GATES], U8, align_bytes=64)
        nc.vector.memset(w_planes[:, 0, :].bitcast(I32), 0)
        bias_rows = const.tile([P, 2 * GATES], BF16)
        nc.vector.memset(bias_rows[:].bitcast(I32), 0)
        ones = const.tile([P, P], BF16)
        nc.vector.memset(ones[:], 1.0)
        neg_half = const.tile([P, ROW_TILES], F32)
        nc.vector.memset(neg_half[:], -0.5)
        nc.vector.memset(w_planes[:, 1:, :].rearrange("p r n -> p (r n)").bitcast(I32), 0)
        identity = const.tile([P, P], F32)
        make_identity(nc, identity[:])

        x_tiles = {}
        w_tiles = {}
        w_halves = {}
        h_sb = const.tile([P, ROW_TILES, HIDDEN], BF16)
        wh_sb = const.tile([P, GATES], U32, align_bytes=64)

        def load_x(i):
            x_sb = x_pool.tile([P, ROW_TILES, ROUND_SIZES[i] * K_PASS], BF16, name="x_sb")
            k_cols = slice(FIRST_PASS[i] * K_PASS, (FIRST_PASS[i] + ROUND_SIZES[i]) * K_PASS)
            nc.sync.dma_start(out=x_sb[:], in_=x_rows[:, :, k_cols])
            x_tiles[i] = x_sb

        def load_w(g):
            w_sb = w_pool.tile([P, GATES], U32, name="w_sb", align_bytes=64)
            nc.sync.dma_start(out=w_sb[:].bitcast(I32), in_=wi_words[g])
            w_tiles[g] = w_sb

        def load_w_half(g_n):
            g, n = g_n
            w_half = w_last_pool.tile([P, N_TILE], U32, name="w_half", align_bytes=64)
            nc.sync.dma_start(out=w_half[:].bitcast(I32), in_=wi_words[g][:, col_tile(n)])
            w_halves[g_n] = w_half

        def load_h(unused):
            nc.sync.dma_start(out=h_sb[:], in_=h_rows)
            nc.sync.dma_start(out=wh_sb[:].bitcast(I32), in_=wh_words[0])

        def load_scale_planes(engine, r):
            for quadrant in range(4):
                engine.dma_start(
                    out=w_planes[32 * quadrant : 32 * quadrant + 16, r, :].bitcast(F32),
                    in_=wi_scales[
                        r * PLANE_GROUP : (r + 1) * PLANE_GROUP, 4 * quadrant : 4 * quadrant + 4, :
                    ],
                )

        queue = [("x", i) for i in range(T_LEAD + 1)]
        for i in range(ROUNDS):
            passes = range(FIRST_PASS[i], FIRST_PASS[i] + ROUND_SIZES[i])
            if ROUND_SIZES[i] < MAX_ROUND:
                queue.extend([("w", g) for g in passes])
            if i + T_LEAD + 1 < ROUNDS:
                if i + T_LEAD + 1 == H_LOAD_BEFORE_X_ROUND:
                    queue.append(("h", 0))
                queue.append(("x", i + T_LEAD + 1))
            if ROUND_SIZES[i] < MAX_ROUND:
                continue
            if i + 1 < ROUNDS:
                queue.extend([("w", g) for g in passes])
            else:
                queue.extend([("half", (g, n)) for n in range(COL_TILES) for g in passes])
        loaders = {"x": load_x, "w": load_w, "half": load_w_half, "h": load_h}

        issued = {"count": 0}

        def issue_loads(sorted_rounds, multiplied_passes):
            for kind, index in queue[issued["count"] :]:
                if kind == "x" and index >= X_BUFS + sorted_rounds:
                    break
                if kind == "w" and index >= W_BUFS + multiplied_passes:
                    break
                loaders[kind](index)
                issued["count"] += 1

        nc.scalar.dma_start(out=bias_rows[0:1, 0:GATES], in_=b_irz.unsqueeze(0))
        nc.scalar.dma_start(out=bias_rows[0:1, GATES : 2 * GATES], in_=b_hrz.unsqueeze(0))
        load_scale_planes(nc.scalar, 0)
        for r in range(1, PLANE_GROUPS):
            load_scale_planes(nc.gpsimd, r)

        table_warmer = const.tile([P, 1], F32)
        nc.scalar.activation(out=table_warmer[:], in_=neg_half[:, 0:1], func=ACT.Sigmoid)

        def sort_words(pool, rows_sb, passes, label):
            sorted_words = pool.tile(
                [P, ROW_TILES * passes, 2, P], F32, name=label + "_sorted_words"
            )
            nc.vector.tensor_copy(
                out=sorted_words[:],
                in_=rows_sb[:].bitcast(F32).rearrange("b m (g p u) -> b (m g) u p", g=passes, u=2),
            )
            return sorted_words

        def turn(pool, sorted_words, passes, label):
            grouped = pool.tile(
                [P, passes * BATCH * PACK], BF16, name=label + "_grouped", align_bytes=64
            )
            grouped_words = grouped[:].bitcast(F32).rearrange("p (g c u) -> p g c u", g=passes, u=2)
            for g in range(passes):
                turned = spare_banks.tile([P, 2, BATCH], F32, name="turned", tag="spare")
                for u in range(2):
                    for m in range(ROW_TILES):
                        nc.tensor.transpose(
                            turned[:, u, m * P : (m + 1) * P],
                            sorted_words[:, m * passes + g, u, :],
                            identity[:],
                        )
                nc.scalar.copy(out=grouped_words[:, g], in_=turned[:].rearrange("p u c -> p c u"))
            return grouped

        def quantise(pool, grouped, passes, label):
            codes = pool.tile([P, passes * BATCH], U32, name=label + "_codes", align_bytes=64)
            scales = pool.tile([P, passes * BATCH], U8, name=label + "_scales", align_bytes=64)
            nc.vector.quantize_mx(out=codes[:].bitcast(FP8X4), scales=scales[:], in_=grouped[:])
            return codes, scales

        def multiply(bank, quantised, j, m, w_cols, plane_cols, first, last):
            codes, scales = quantised
            rows = slice(j * BATCH + m * P, j * BATCH + (m + 1) * P)
            nc.tensor.matmul_mx(
                out=bank[:],
                lhsT=codes[:, rows].bitcast(FP8X4),
                lhsT_scale=scales[:, rows],
                rhs=w_cols.bitcast(FP8X4),
                rhs_scale=plane_cols,
                start=first,
                stop=last,
            )

        def new_rows(label):
            return [rows_pool.tile([P, GATES], F32, name=label) for m in range(ROW_TILES)]

        def new_stats():
            return [
                stat_pool.tile([P, COL_TILES, 6], F32, name="stats") for m in range(ROW_TILES)
            ]

        def add_bias(v, sums, bias_cols, m, n):
            nc.vector.tensor_tensor(
                out=v[m][:, col_tile(n)], in0=sums[m][n][:], in1=bias_cols[:, col_tile(n)],
                op=ALU.add,
            )

        def measure(stats, v, m, n):
            nc.vector.bn_stats(out=stats[m][:, n, :], in_=v[m][:, col_tile(n)])

        def mean_and_rstd(stats):
            mean_var = stat_pool.tile([P, ROW_TILES, 2], F32, name="mean_var")
            for m in range(ROW_TILES):
                nc.vector.bn_aggr(
                    out=mean_var[:, m, :], in_=stats[m][:].rearrange("p n s -> p (n s)")
                )
            var_eps = stat_pool.tile([P, ROW_TILES], F32, name="var_eps")
            nc.vector.tensor_scalar_add(var_eps[:], mean_var[:, :, 1], EPS)
            rstd = stat_pool.tile([P, ROW_TILES], F32, name="rstd")
            nc.gpsimd.tensor_tensor(out=rstd[:], in0=var_eps[:], in1=neg_half[:], op=ALU.pow)
            return mean_var, rstd

        def shift_of(mean_var, rstd):
            shift = stat_pool.tile([P, ROW_TILES], F32, name="shift")
            nc.vector.scalar_tensor_tensor(
                out=shift[:], in0=mean_var[:, :, 0], scalar=-1.0, in1=rstd[:],
                op0=ALU.mult, op1=ALU.mult,
            )
            return shift

        issue_loads(0, 0)

        x_sorted = {i: sort_words(quant_pool, x_tiles[i], ROUND_SIZES[i], "x") for i in range(2)}
        x_grouped = {i: turn(quant_pool, x_sorted[i], ROUND_SIZES[i], "x") for i in range(2)}
        x_quantised = {0: quantise(codes_pool, x_grouped[0], ROUND_SIZES[0], "x")}
        x_sorted[2] = sort_words(quant_pool, x_tiles[2], ROUND_SIZES[2], "x")
        x_quantised[1] = quantise(codes_pool, x_grouped[1], ROUND_SIZES[1], "x")

        bias = const.tile([P, 2 * GATES], F32)
        for c in range(2 * COL_TILES):
            spread = spare_banks.tile([P, N_TILE], F32, name="spread", tag="spare")
            nc.tensor.matmul(
                out=spread[:], lhsT=ones[:], rhs=bias_rows[:, col_tile(c)], start=True, stop=True
            )
            nc.scalar.copy(out=bias[:, col_tile(c)], in_=spread[:])
        x_bias = bias[:, 0:GATES]
        h_bias = bias[:, GATES : 2 * GATES]

        x_sums = [
            [sum_banks.tile([P, N_TILE], F32, name="sums_%d_%d" % (m, n)) for n in range(COL_TILES)]
            for m in range(ROW_TILES)
        ]
        h_state = {}
        for i in range(ROUNDS):
            size = ROUND_SIZES[i]
            issue_loads(i + T_LEAD + 1, FIRST_PASS[i])
            if i == H_PLANE_ROUND:
                for quadrant in range(4):
                    nc.scalar.dma_start(
                        out=w_planes[32 * quadrant : 32 * quadrant + 4, PLANE_GROUPS, :].bitcast(F32),
                        in_=wh_scales[0, 4 * quadrant : 4 * quadrant + 4, :],
                    )
            ahead = i + T_LEAD
            if ahead + 1 < ROUNDS:
                x_sorted[ahead + 1] = sort_words(
                    quant_pool, x_tiles[ahead + 1], ROUND_SIZES[ahead + 1], "x"
                )
            if i == H_ROUND - 2:
                h_state["sorted"] = sort_words(const, h_sb, 1, "h")
            if ahead < ROUNDS:
                x_grouped[ahead] = turn(quant_pool, x_sorted[ahead], ROUND_SIZES[ahead], "x")
            if i == H_ROUND - 1:
                h_state["grouped"] = turn(const, h_state["sorted"], 1, "h")
            if ahead < ROUNDS:
                x_quantised[ahead] = quantise(codes_pool, x_grouped[ahead], ROUND_SIZES[ahead], "x")
            if i == H_ROUND - 1:
                h_state["quantised"] = quantise(const, h_state["grouped"], 1, "h")

            if i + 1 < ROUNDS:
                steps = [
                    (j, m, n)
                    for j in range(size) for n in range(COL_TILES) for m in range(ROW_TILES)
                ]
            else:
                steps = [
                    (j, m, n)
                    for n in range(COL_TILES) for m in range(ROW_TILES) for j in range(size)
                ]
            for s, (j, m, n) in enumerate(steps):
                if i == H_ROUND and s == len(steps) // 2:
                    h_sums = [
                        [
                            spare_banks.tile([P, N_TILE], F32, name="h_sums", tag="spare")
                            for nn in range(COL_TILES)
                        ]
                        for m in range(ROW_TILES)
                    ]
                    for nn in range(COL_TILES):
                        for mm in range(ROW_TILES):
                            multiply(
                                h_sums[mm][nn], h_state["quantised"], 0, mm,
                                wh_sb[:, col_tile(nn)], w_planes[:, PLANE_GROUPS, col_tile(nn)],
                                True, True,
                            )
                g = FIRST_PASS[i] + j
                multiply(
                    x_sums[m][n], x_quantised[i], j, m,
                    w_tiles[g][:, col_tile(n)] if i + 1 < ROUNDS else w_halves[(g, n)][:],
                    w_planes[4 * (g % PLANE_GROUP) : P, g // PLANE_GROUP, col_tile(n)],
                    g == 0, g == X_PASSES - 1,
                )
            if i == H_ROUND:
                h_v = new_rows("v")
                h_stats = new_stats()
                for n in range(COL_TILES):
                    for m in range(ROW_TILES):
                        add_bias(h_v, h_sums, h_bias, m, n)
                for n in range(COL_TILES):
                    for m in range(ROW_TILES):
                        measure(h_stats, h_v, m, n)
                h_mean_var, h_rstd = mean_and_rstd(h_stats)
            if i == H_NORM_ROUND:
                h_norm = new_rows("h_norm")
                h_shift = shift_of(h_mean_var, h_rstd)
                for m in range(ROW_TILES):
                    nc.vector.tensor_scalar(
                        out=h_norm[m][:], in0=h_v[m][:],
                        scalar1=h_rstd[:, m : m + 1], scalar2=h_shift[:, m : m + 1],
                        op0=ALU.mult, op1=ALU.add,
                    )

        x_v = new_rows("v")
        z = new_rows("z")
        sum_v = stat_pool.tile([P, ROW_TILES, COL_TILES], F32, name="sum_v")
        sum_sq = stat_pool.tile([P, ROW_TILES, COL_TILES], F32, name="sum_sq")
        neg_pivot = stat_pool.tile([P, ROW_TILES], F32, name="neg_pivot")
        first_part = stat_pool.tile([P, ROW_TILES], F32, name="first_part")
        off_pivot = stat_pool.tile([P, ROW_TILES], F32, name="off_pivot")
        neg_square = stat_pool.tile([P, ROW_TILES], F32, name="neg_square")
        known_part = stat_pool.tile([P, ROW_TILES], F32, name="known_part")
        x_var_eps = stat_pool.tile([P, ROW_TILES], F32, name="var_eps")
        x_rstd = stat_pool.tile([P, ROW_TILES], F32, name="rstd")

        def step_off_pivot(m):
            nc.vector.tensor_tensor(
                out=off_pivot[:, m : m + 1], in0=sum_v[:, m, 1:2], in1=sum_v[:, m, 0:1],
                op=ALU.subtract,
            )

        def step_neg_square(m):
            nc.vector.scalar_tensor_tensor(
                out=neg_square[:, m : m + 1], in0=off_pivot[:, m : m + 1],
                scalar=-1.0 / (GATES * GATES), in1=off_pivot[:, m : m + 1],
                op0=ALU.mult, op1=ALU.mult,
            )

        def step_known_part(m):
            nc.vector.tensor_tensor(
                out=known_part[:, m : m + 1], in0=first_part[:, m : m + 1],
                in1=neg_square[:, m : m + 1], op=ALU.add,
            )

        def step_rstd(m):
            nc.vector.scalar_tensor_tensor(
                out=x_var_eps[:, m : m + 1], in0=sum_sq[:, m, 1:2], scalar=1.0 / GATES,
                in1=known_part[:, m : m + 1], op0=ALU.mult, op1=ALU.add,
            )
            nc.gpsimd.tensor_tensor(
                out=x_rstd[:, m : m + 1], in0=x_var_eps[:, m : m + 1], in1=neg_half[:, m : m + 1],
                op=ALU.pow,
            )

        for n in range(COL_TILES):
            for m in range(ROW_TILES):
                cols = col_tile(n)
                if (m, n) == (ROW_TILES - 1, COL_TILES - 1):
                    nc.vector.tensor_scalar(
                        out=first_part[:], in0=sum_sq[:, :, 0], scalar1=1.0 / GATES, scalar2=EPS,
                        op0=ALU.mult, op1=ALU.add,
                    )
                    step_off_pivot(0)
                nc.vector.scalar_tensor_tensor(
                    out=x_v[m][:, cols], in0=x_sums[m][n][:], scalar=1.0, in1=x_bias[:, cols],
                    op0=ALU.mult, op1=ALU.add, accum_out=sum_v[:, m, n : n + 1],
                )
                if n == 0:
                    nc.vector.tensor_scalar_mul(
                        neg_pivot[:, m : m + 1], sum_v[:, m, 0:1], -1.0 / N_TILE
                    )
                nc.scalar.activation(
                    out=z[m][:, cols], in_=x_v[m][:, cols], func=ACT.Square,
                    bias=neg_pivot[:, m : m + 1], accum_out=sum_sq[:, m, n : n + 1],
                )
        step_neg_square(0)
        step_off_pivot(1)
        step_known_part(0)
        step_neg_square(1)
        step_rstd(0)
        step_known_part(1)
        step_rstd(1)
        row_sum = stat_pool.tile([P, ROW_TILES], F32, name="row_sum")
        nc.vector.tensor_tensor(
            out=row_sum[:], in0=sum_v[:, :, 0], in1=sum_v[:, :, 1], op=ALU.add
        )
        x_shift = stat_pool.tile([P, ROW_TILES], F32, name="shift")
        gates = new_rows("gates")
        for m in range(ROW_TILES):
            for n in range(COL_TILES):
                cols = col_tile(n)
                nc.vector.scalar_tensor_tensor(
                    out=z[m][:, cols], in0=x_v[m][:, cols], scalar=x_rstd[:, m : m + 1],
                    in1=h_norm[m][:, cols], op0=ALU.mult, op1=ALU.add,
                )
                if n == 0:
                    nc.vector.scalar_tensor_tensor(
                        out=x_shift[:, m : m + 1], in0=row_sum[:, m : m + 1], scalar=-1.0 / GATES,
                        in1=x_rstd[:, m : m + 1], op0=ALU.mult, op1=ALU.mult,
                    )
                nc.scalar.activation(
                    out=gates[m][:, cols], in_=z[m][:, cols], func=ACT.Sigmoid,
                    bias=x_shift[:, m : m + 1],
                )
                nc.sync.dma_start(out=out_rows[:, m, cols], in_=gates[m][:, cols])
